import numpy as np
import ml_dtypes


def mxq(x, axis, fmt="e4m3"):
    dtype, down = {"e4m3": (ml_dtypes.float8_e4m3fn, 7), "e5m2": (ml_dtypes.float8_e5m2, 14)}[fmt]
    v = np.moveaxis(np.asarray(x, np.float32).astype(ml_dtypes.bfloat16).astype(np.float64), axis, -1)
    blocks = v.reshape(v.shape[:-1] + (-1, 32))
    amax = np.abs(blocks).max(-1, keepdims=True)
    byte = np.maximum(np.where(amax > 0, np.frexp(amax)[1] - 1 + 127, 0) - down, 1)
    scale = np.exp2(byte - 127.0)
    codes = (blocks / scale).astype(np.float32).astype(dtype).astype(np.float64)
    return np.moveaxis((codes * scale).reshape(v.shape), -1, axis)


WIDE = False


def mx_kscale(k):
    if not WIDE:
        return np.ones(k)
    levels = np.array([10, -10, 5, -5, 0])
    if k % 512:
        return np.exp2(np.random.permutation(np.resize(levels, k // 32))).repeat(32)
    a = np.empty((k // 512, 16))
    for p in range(k // 512):
        a[p, :8] = np.random.permutation(np.resize(levels, 8))
        for g in range(8):
            far = levels[np.abs(levels - a[p, g]) >= 10]
            a[p, g + 8] = far[np.random.randint(len(far))]
    return np.exp2(a.ravel()).repeat(32)


BF16 = ml_dtypes.bfloat16


def bf(x):
    return np.asarray(x, np.float32).astype(BF16)


def f64(x):
    return np.asarray(x).astype(np.float64)


E2M1 = np.array([0.0, 0.5, 1.0, 1.5, 2.0, 3.0, 4.0, 6.0, -0.0, -0.5, -1.0, -1.5, -2.0, -3.0, -4.0, -6.0])


def pack_weight(w, fmt):
    k, n = w.shape
    w = f64(bf(w)).reshape(k // 32, 32, n)
    amax = np.abs(w).max(1)
    if fmt == "e4m3":
        byte = np.frexp(amax)[1] - 1 + 127 - 7
    else:
        mant, ex = np.frexp(amax / 6.0)
        byte = np.where(mant > 0.5, ex, ex - 1) + 127
    byte = np.clip(np.where(amax > 0, byte, 1), 1, 254)
    scaled = (w * np.exp2(127.0 - byte)[:, None, :]).reshape(k, n).astype(np.float32)
    by_word = np.ascontiguousarray(scaled.reshape(k // 512, 128, 4, n).transpose(0, 1, 3, 2))
    if fmt == "e4m3":
        words = by_word.astype(ml_dtypes.float8_e4m3fn).view(np.uint8)
    else:
        c = by_word.astype(ml_dtypes.float4_e2m1fn).view(np.uint8) & 0xF
        words = c[..., 0::2] | (c[..., 1::2] << 4)
    return np.ascontiguousarray(words), np.ascontiguousarray(byte.astype(np.uint8).reshape(k // 512, 16, n))


def unpack_weight(words, scales, fmt):
    g, p, n, _ = words.shape
    if fmt == "e4m3":
        vals = np.ascontiguousarray(words).view(ml_dtypes.float8_e4m3fn).astype(np.float64)
    else:
        nib = np.empty((g, p, n, 4), np.uint8)
        nib[..., 0::2] = words & 0xF
        nib[..., 1::2] = words >> 4
        vals = E2M1[nib]
    vals = vals * np.repeat(np.exp2(scales.astype(np.float64) - 127.0), 8, axis=1)[..., None]
    return vals.transpose(0, 1, 3, 2).reshape(g * 512, n)
def pack4(w):
    words, scales = pack_weight(w, "e2m1")
    return words.reshape(words.shape[0], 128, -1), scales


def unpack4(words, scales):
    return unpack_weight(words.reshape(words.shape[0], 128, -1, 2), scales, "e2m1")


B, D, K, Q, G0, G1, F1, F2, OUT = 128, 12, 7, 512, 512, 512, 512, 1024, 16


def draw0():
    s, r, t = mx_kscale(G0), mx_kscale(Q), mx_kscale(G1)
    sr = np.concatenate([s, r])
    u_i = bf(np.random.standard_normal((B, D, G0)) * np.sqrt(0.5) * s)
    u_j = bf(np.random.standard_normal((B, D, G0)) * np.sqrt(0.5) * s)
    g0_b = bf(np.random.standard_normal(G0) * 0.3 * s)
    qst = bf(np.random.standard_normal((B, Q)) * 0.5 * r)
    g1_w_words, g1_w_scales = pack4(np.random.standard_normal((G0 + Q, G1)) * 0.15 / np.sqrt(G0 + Q) / sr[:, None] * t)
    g1_b = bf(np.random.standard_normal(G1) * 0.03 * t)
    f1_w_words, f1_w_scales = pack4(np.random.standard_normal((G1, F1)) * 0.125 / np.sqrt(G1) / t[:, None])
    f1_b = bf(np.random.standard_normal(F1) * 0.3)
    return {"u_i": u_i,
            "u_j": u_j,
            "g0_b": g0_b,
            "qst": qst,
            "g1_w_words": g1_w_words,
            "g1_w_scales": g1_w_scales,
            "g1_b": g1_b,
            "f1_w_words": f1_w_words,
            "f1_w_scales": f1_w_scales,
            "f1_b": f1_b}


def core(u_i, u_j, g0_b, qst, g1_w_words, g1_w_scales, g1_b, f1_w_words, f1_w_scales, f1_b):
    w = unpack4(g1_w_words, g1_w_scales)
    h = np.maximum(f64(u_i)[:, None, :, :] + f64(u_j)[:, :, None, :] + f64(g0_b), 0.0)
    zp = (mxq(h.reshape(B * D * D, G0), 1, "e4m3") @ w[:G0]).reshape(B, D, D, G1)
    zq = mxq(f64(qst), 1, "e4m3") @ w[G0:]
    z = zp + zq[:, None, None, :] + f64(g1_b)
    x_g = np.maximum(z, 0.0).sum(axis=(1, 2))
    return np.maximum((mxq(x_g, 1, "e4m3") @ unpack4(f1_w_words, f1_w_scales)) + f64(f1_b), 0.0)


def e4m3fn_bytes(y):
    return np.clip(np.asarray(y, np.float64), -448.0, 448.0).astype(np.float32).astype(ml_dtypes.float8_e4m3fn).view(np.uint8)


def e4m3fn_values(b):
    return np.asarray(b, np.uint8).view(ml_dtypes.float8_e4m3fn).astype(np.float64)


def setup_inputs():
    d = draw0()
    x0 = np.asarray(d['qst']).astype(np.float64)
    s = (np.max(np.abs(x0), axis=(0,), keepdims=True) / 448.0).astype(np.float32)
    out = {}
    for k, v in d.items():
        if k == 'qst':
            out['qst_bytes'] = e4m3fn_bytes(x0 / s.astype(np.float64))
            out['qst_scale'] = s
        else:
            out[k] = v
    return out


def reference(u_i, u_j, g0_b, qst_bytes, qst_scale, g1_w_words, g1_w_scales, g1_b, f1_w_words, f1_w_scales, f1_b):
    return core(u_i, u_j, g0_b, e4m3fn_values(qst_bytes) * qst_scale.astype(np.float64), g1_w_words, g1_w_scales, g1_b, f1_w_words, f1_w_scales, f1_b)

@@ -1,0 +1,395 @@
+from contextlib import ExitStack
+
+import concourse.mybir as mybir
+from concourse.masks import make_identity
+
+F32 = mybir.dt.float32
+BF16 = mybir.dt.bfloat16
+I32 = mybir.dt.int32
+U32 = mybir.dt.uint32
+U8 = mybir.dt.uint8
+FP8 = mybir.dt.float8_e4m3fn
+FP8X4 = mybir.dt.float8_e4m3fn_x4
+FP4X4 = mybir.dt.float4_e2m1fn_x4
+ALU = mybir.AluOpType
+ACT = mybir.ActivationFunctionType
+
+P = 128
+B, D, K = 128, 12, 512
+PAIRS = D * D
+ROWS = B * PAIRS
+FLOPS = 2 * ROWS * K * K + 2 * (2 * B * K * K)
+
+PER_SLOT = 3
+SLOT = 448
+BLOCK = 8 * SLOT
+N_SLOTS = 43
+N_TE = 17
+N_TE_SAMPLES = N_TE * PER_SLOT
+PER_TILE = 9
+N_TILES = 9
+LEAD = 4
+SHIFTED = K - 3
+G_COUNT = (2, 4, 4, 4, 4, 4, 4, 4, 2)
+G_SPLIT = 3
+VEC_BANKS = [(k, 3) for k in range(4, 40) if k % 3 == 1] + [(41, 3), (42, 1), (42, 3)]
+LOAD_RUNS = ((0, 3), (3, 9), (9, 18), (18, 33), (33, 51))
+
+
+def slot_plan():
+    te = [("te", [PER_SLOT * i + s for s in range(PER_SLOT)]) for i in range(N_TE)]
+    ve = []
+    b = N_TE_SAMPLES
+    while b < B:
+        ve.append(("ve", list(range(b, min(b + PER_SLOT, B)))))
+        b += PER_SLOT
+    order = [ve[0], te[0], te[1]]
+    n_te, n_ve = 2, 1
+    while n_te + n_ve < N_SLOTS:
+        if n_te < N_TE and (n_te - 2) * len(ve) < n_ve * (N_TE - 2):
+            order.append(te[n_te])
+            n_te += 1
+        else:
+            order.append(ve[n_ve])
+            n_ve += 1
+    return order
+
+
+def quantize_plan():
+    widths = [256, 128, 64] * 2 + [512] * 5 + [128]
+    widths += [512] * (4 * 7) + [512, 512, 256]
+    plan, at = [], 0
+    for w in widths:
+        plan.append((at, w))
+        at += w
+    return plan
+
+
+def tile_rn_pa_w4_kernel(tc, u_i, u_j, g0_b, qst_bytes, qst_scale, g1_w_words, g1_w_scales, g1_b,
+                                     f1_w_words, f1_w_scales, f1_b, out):
+    nc = tc.nc
+    with ExitStack() as ctx:
+        keep = ctx.enter_context(tc.tile_pool(name="keep", bufs=1))
+        junk_pool = ctx.enter_context(tc.tile_pool(name="junk_pool", bufs=6))
+        z_pool = ctx.enter_context(tc.psum_pool(name="z_pool", bufs=4))
+        ph_pool = ctx.enter_context(tc.psum_pool(name="ph_pool", bufs=2))
+        xt_pool = ctx.enter_context(tc.psum_pool(name="xt_pool", bufs=2))
+        ctx.enter_context(tc.manual_schedule())
+
+        ui_rows = u_i.rearrange("b d k -> (b d) k")
+        uj_rows = u_j.rearrange("b d k -> (b d) k")
+
+        te_rows = keep.tile([P, N_TE_SAMPLES, K], BF16, align_bytes=64)
+        ve_i = keep.tile([P, N_TILES, K], BF16, align_bytes=64)
+        ve_j = keep.tile([P, N_TILES, K], BF16, align_bytes=64)
+        g0_t = keep.tile([P, 4], BF16, align_bytes=64)
+        g1_t = keep.tile([P, 4], BF16, align_bytes=64)
+        q_raw = keep.tile([P, K], U8, align_bytes=64)
+        q_scale = keep.tile([P, K], F32, align_bytes=64)
+        w_raw = keep.tile([P, 2, 1024], U8, align_bytes=64)
+        ws_raw = keep.tile([P, 2, K], U8, align_bytes=64)
+        w_perm = keep.tile([P, 2, 4, 256], U8, align_bytes=64)
+        ws_perm = keep.tile([P, 2, 4, P], U8, align_bytes=64)
+        f1_words = keep.tile([P, 1024], U8, align_bytes=64)
+        f1_scales = keep.tile([P, K], U8, align_bytes=64)
+        f1_bias = keep.tile([P, K], BF16, align_bytes=64)
+        ident = keep.tile([P, P], F32, align_bytes=64)
+        ident_bf = keep.tile([P, P], BF16, align_bytes=64)
+        sel = keep.tile([P, PAIRS, 4], BF16, align_bytes=64)
+        zeros = keep.tile([P, PAIRS], F32, align_bytes=64)
+        h = keep.tile([P, 2 * BLOCK, 4], BF16, align_bytes=64)
+        codes = keep.tile([P, 2 * BLOCK], U32, align_bytes=64)
+        scales = keep.tile([P, 2 * BLOCK], U8, align_bytes=64)
+        ujg = keep.tile([P, 2, PER_TILE * D, 4], F32, align_bytes=64)
+        uis = keep.tile([P, 2, PER_TILE * D, 4], BF16, align_bytes=64)
+        bias = keep.tile([P, 4, B], F32, align_bytes=64)
+        acc = keep.tile([P, B, 4], F32, align_bytes=64)
+        xg = keep.tile([P, B, 4], BF16, align_bytes=64)
+        xg_codes = keep.tile([P, B], U32, align_bytes=64)
+        xg_scales = keep.tile([P, B], U8, align_bytes=64)
+        result = keep.tile([P, K], F32, align_bytes=64)
+        q_val = keep.tile([P, K], BF16, align_bytes=64)
+        q_int = keep.tile([P, K], BF16, align_bytes=64)
+        q_codes = keep.tile([P, B], U32, align_bytes=64)
+        q_scales = keep.tile([P, B], U8, align_bytes=64)
+        warm = keep.tile([P, 1], F32)
+
+        nc.vector.memset(ws_raw[:].rearrange("p g n -> p (g n)").bitcast(I32), 0)
+        nc.vector.memset(f1_scales[:].bitcast(I32), 0)
+        make_identity(nc, ident[:])
+
+        def load_te(s0, s1, queues):
+            for t in range(4):
+                queues[t % len(queues)].dma_start(
+                    out=te_rows[32 * t:32 * t + D, s0:s1, 0:SHIFTED],
+                    in_=ui_rows[D * s0:D * s1, t:t + SHIFTED].rearrange("(s r) k -> r s k", r=D))
+                for (p0, n, shift) in ((D, D, 0), (2 * D, 7, 1)):
+                    src = uj_rows[D * (s0 + shift):D * (s1 + shift), t:t + SHIFTED].rearrange("(s r) k -> r s k", r=D)
+                    queues[t % len(queues)].dma_start(out=te_rows[32 * t + p0:32 * t + p0 + n, s0:s1, 0:SHIFTED],
+                                                      in_=src[0:n])
+
+        def ve_row0(v):
+            return min((N_TE_SAMPLES + PER_TILE * v) * D, B * D - P)
+
+        def load_ve(v, queue):
+            r0 = ve_row0(v)
+            queue.dma_start(out=ve_j[:, v, :], in_=uj_rows[r0:r0 + P, :])
+            queue.dma_start(out=ve_i[:, v, :], in_=ui_rows[r0:r0 + P, :])
+
+        def load_g0(s0, s1):
+            for t in range(4):
+                nc.sync.dma_start(
+                    out=te_rows[32 * t + 31:32 * t + 32, s0:s1, 0:SHIFTED],
+                    in_=g0_b[t:t + SHIFTED].partition_broadcast(1).unsqueeze(1).to_broadcast([1, s1 - s0, SHIFTED]))
+
+        load_ve(0, nc.scalar)
+        nc.scalar.dma_start(out=g0_t[:], in_=g0_b.rearrange("(p t) -> p t", t=4))
+        for q in range(4):
+            nc.sync.dma_start(out=ws_raw[32 * q:32 * q + 4, :, :].bitcast(I32),
+                              in_=g1_w_scales[:, 4 * q:4 * q + 4, :].rearrange("g r n -> r g n").bitcast(I32))
+        nc.sync.dma_start(out=w_raw[:].bitcast(I32), in_=g1_w_words.rearrange("g p n -> p g n").bitcast(I32))
+        load_te(LOAD_RUNS[0][0], LOAD_RUNS[0][1], [nc.scalar, nc.sync])
+        load_g0(LOAD_RUNS[0][0], LOAD_RUNS[0][1])
+        nc.sync.dma_start(out=q_raw[:], in_=qst_bytes)
+        nc.sync.dma_start(out=q_scale[:], in_=qst_scale.rearrange("o k -> (o k)").partition_broadcast(P))
+        nc.sync.dma_start(out=g1_t[:], in_=g1_b.rearrange("(p t) -> p t", t=4))
+        load_te(LOAD_RUNS[1][0], LOAD_RUNS[1][1], [nc.sync])
+        load_g0(LOAD_RUNS[1][0], N_TE_SAMPLES)
+        load_ve(1, nc.sync)
+        load_te(LOAD_RUNS[2][0], LOAD_RUNS[2][1], [nc.sync])
+        load_ve(2, nc.sync)
+        load_ve(3, nc.sync)
+        load_te(LOAD_RUNS[3][0], LOAD_RUNS[3][1], [nc.sync])
+        load_ve(4, nc.sync)
+        load_ve(5, nc.sync)
+        load_te(LOAD_RUNS[4][0], LOAD_RUNS[4][1], [nc.sync])
+        for v in range(6, N_TILES):
+            load_ve(v, nc.sync)
+        for q in range(4):
+            nc.sync.dma_start(out=f1_scales[32 * q:32 * q + 4, :].bitcast(I32),
+                              in_=f1_w_scales[0, 4 * q:4 * q + 4, :].bitcast(I32))
+        nc.sync.dma_start(out=f1_words[:].bitcast(I32), in_=f1_w_words[0].bitcast(I32))
+        nc.sync.dma_start(out=f1_bias[:], in_=f1_b.partition_broadcast(P))
+
+        nc.scalar.activation(out=warm[:], in_=ident[:, 0:1], func=ACT.Relu)
+        nc.vector.tensor_copy(out=ident_bf[:], in_=ident[:])
+        by_t = ident_bf[:].rearrange("p (t r) -> p r t", t=4)
+        sel4 = sel[:].rearrange("p (a c) t -> p a c t", a=D)
+        nc.vector.tensor_tensor(out=sel4, in0=by_t[:, 0:D, :].unsqueeze(1).to_broadcast([P, D, D, 4]),
+                                in1=by_t[:, D:2 * D, :].unsqueeze(2).to_broadcast([P, D, D, 4]), op=ALU.add)
+        nc.vector.tensor_tensor(out=sel[:], in0=sel[:], in1=by_t[:, 31, :].unsqueeze(1).to_broadcast([P, PAIRS, 4]), op=ALU.add)
+        nc.vector.memset(zeros[:], 0.0)
+        nc.vector.memset(h[:].rearrange("p (s n) t -> p s (n t)", n=SLOT)[:, :, PER_SLOT * PAIRS * 4:], 0.0)
+
+        def permute(engine, g):
+            nc.vector.tensor_copy(out=ws_perm[:, g], in_=ws_raw[:, g].rearrange("p (m j) -> p j m", j=4))
+            engine.tensor_copy(out=w_perm[:, g].rearrange("p j (m e) -> p j m e", e=2),
+                               in_=w_raw[:, g].rearrange("p (m j e) -> p j m e", j=4, e=2))
+
+        permute(nc.vector, 0)
+        permute(nc.gpsimd, 1)
+
+        slots = slot_plan()
+        assert len(slots) == N_SLOTS
+
+        def column(k):
+            return (k // 8) % 2 * BLOCK + k % 8 * SLOT
+
+        slot_of = {}
+        for k, (kind, samples) in enumerate(slots):
+            for s, b in enumerate(samples):
+                slot_of[b] = column(k) + s * PAIRS
+
+        xts = {}
+
+        def tile_samples(v):
+            b0 = N_TE_SAMPLES + PER_TILE * v
+            return list(range(b0, min(b0 + PER_TILE, B)))
+
+        def on_gpsimd(b):
+            v = (b - N_TE_SAMPLES) // PER_TILE
+            samples = tile_samples(v)
+            return b >= samples[-1] + 1 - G_COUNT[v]
+
+        def sum_pairs(engine, b, a0, a1, u_i_rows, u_j_rows):
+            n = a1 - a0
+            lo = slot_of[b]
+            engine.tensor_tensor(
+                out=h[:, lo + a0 * D:lo + a1 * D, :].rearrange("p (a c) t -> p a c t", a=n),
+                in0=u_i_rows.unsqueeze(1).to_broadcast([P, n, D, 4]),
+                in1=u_j_rows[:, a0:a1, :].unsqueeze(2).to_broadcast([P, n, D, 4]), op=ALU.add)
+
+        def prep(v):
+            xt = xt_pool.tile([P, 2, P, 2], F32, name="xt")
+            xts[v] = xt
+            for i, src in ((1, ve_j), (0, ve_i)):
+                words = src[:, v, :].bitcast(F32)
+                for u in (0, 1):
+                    nc.tensor.transpose(xt[:, i, :, u], words[:, u:K // 2:2], ident[:])
+            samples = tile_samples(v)
+            off = samples[0] * D - ve_row0(v)
+            n = len(samples) * D
+            nc.vector.tensor_tensor(
+                out=ujg[:, v % 2, 0:n, :],
+                in0=xt[:, 1, off:off + n, :].rearrange("p r u -> p (r u)").bitcast(BF16).rearrange("p (r t) -> p r t", t=4),
+                in1=g0_t[:].unsqueeze(1).to_broadcast([P, n, 4]), op=ALU.add)
+            n_g = G_COUNT[v] * D
+            if n_g:
+                nc.vector.tensor_copy(out=uis[:, v % 2, n - n_g:n, :].rearrange("p r t -> p (r t)").bitcast(F32),
+                                      in_=xt[:, 0, off + n - n_g:off + n, :].rearrange("p r u -> p (r u)"))
+                for i, b in enumerate(samples):
+                    if on_gpsimd(b):
+                        for a in range(0, D, D // G_SPLIT):
+                            sum_pairs(nc.gpsimd, b, a, a + D // G_SPLIT, uis[:, v % 2, i * D:(i + 1) * D, :],
+                                      ujg[:, v % 2, i * D:(i + 1) * D, :])
+
+        state = {"prepped": 0}
+
+        def te_unit(k, unit, samples):
+            ph = ph_pool.tile([P, 1024], BF16, name="ph")
+            for r in range(3):
+                half = 3 * unit + r
+                b = samples[half // 2]
+                nc.tensor.matmul(ph[:, 288 * r:288 * (r + 1)],
+                                 lhsT=te_rows[:, b, :].rearrange("p (m t) -> p t m", t=4)[:, 0, :],
+                                 rhs=sel[:, 72 * (half % 2):72 * (half % 2) + 72, :].rearrange("p n t -> p (n t)"),
+                                 start=True, stop=True)
+            lo = column(k) + 216 * unit
+            dst = h[:, lo:lo + 216, :].rearrange("p n t -> p (n t)")
+            if k < 4 and unit == 1:
+                nc.scalar.activation(out=dst, in_=ph[:, 0:864], func=ACT.Relu)
+            else:
+                nc.vector.tensor_scalar_max(dst, ph[:, 0:864], 0.0)
+
+        def ve_sample(b):
+            v = (b - N_TE_SAMPLES) // PER_TILE
+            if (b - N_TE_SAMPLES) % PER_TILE == 3 and state["prepped"] == v + 1 and v + 1 < N_TILES:
+                prep(v + 1)
+                state["prepped"] = v + 2
+            if not on_gpsimd(b):
+                off = b * D - ve_row0(v)
+                ui_bf = xts[v][:, 0, off:off + D, :].rearrange("p r u -> p (r u)").bitcast(BF16)
+                i = (b - N_TE_SAMPLES) % PER_TILE
+                sum_pairs(nc.vector, b, 0, D, ui_bf.rearrange("p (c t) -> p c t", t=4), ujg[:, v % 2, i * D:(i + 1) * D, :])
+
+        def relu(k):
+            if slots[k][0] == "ve":
+                n = len(slots[k][1]) * PAIRS
+                flat = h[:, column(k):column(k) + n, :].rearrange("p n t -> p (n t)")
+                nc.vector.tensor_scalar_max(flat, flat, 0.0)
+
+        def production(k):
+            kind, samples = slots[k]
+            if kind == "te":
+                return [lambda k=k, unit=unit, samples=samples: te_unit(k, unit, samples) for unit in (0, 1)]
+            return [lambda b=b: ve_sample(b) for b in samples]
+
+        plan = quantize_plan()
+
+        def quantize(piece):
+            at, width = plan[piece]
+            lo = at // BLOCK % 2 * BLOCK + at % BLOCK
+            nc.vector.quantize_mx(out=codes[:, lo:lo + width].bitcast(FP8X4), scales=scales[:, lo:lo + width],
+                                  in_=h[:, lo:lo + width, :].rearrange("p n t -> p (n t)"))
+
+        def last_slot(piece):
+            at, width = plan[piece]
+            return min((at + width - 1) // SLOT, N_SLOTS - 1)
+
+        def z_and_reduce(k, j):
+            samples = slots[k][1]
+            z = z_pool.tile([P, 512], F32, name="z")
+            second = 192 if len(samples) == PER_SLOT else 64
+            for w in (0, second):
+                lo = column(k) + w
+                nc.tensor.matmul_mx(out=z[:, w:w + 256], lhsT=w_perm[:, 0, j, :].bitcast(FP4X4), lhsT_scale=ws_perm[:, 0, j, :],
+                                    rhs=codes[:, lo:lo + 256].bitcast(FP8X4), rhs_scale=scales[:, lo:lo + 256],
+                                    start=True, stop=True)
+            for s, b in enumerate(samples):
+                junk = junk_pool.tile([P, PAIRS], F32, name="junk")
+                src = z[:, s * PAIRS:(s + 1) * PAIRS]
+                if (k, j) in VEC_BANKS:
+                    nc.vector.scalar_tensor_tensor(out=junk[:], in0=src, scalar=bias[:, j, b:b + 1], in1=zeros[:],
+                                                   op0=ALU.add, op1=ALU.max, accum_out=acc[:, b, j:j + 1])
+                else:
+                    nc.scalar.activation(out=junk[:], in_=src, func=ACT.Relu, bias=bias[:, j, b:b + 1],
+                                         accum_out=acc[:, b, j:j + 1])
+
+        def question():
+            nc.vector.tensor_tensor(out=q_val[:], in0=q_raw[:].bitcast(FP8), in1=q_scale[:], op=ALU.mult)
+            xq = xt_pool.tile([P, 2, P, 2], F32, name="xt")
+            words = q_val[:].bitcast(F32)
+            for u in (0, 1):
+                nc.tensor.transpose(xq[:, 0, :, u], words[:, u:K // 2:2], ident[:])
+            nc.vector.tensor_copy(out=q_int[:].bitcast(F32), in_=xq[:, 0].rearrange("p r u -> p (r u)"))
+            nc.vector.quantize_mx(out=q_codes[:].bitcast(FP8X4), scales=q_scales[:], in_=q_int[:])
+            zq = z_pool.tile([P, 512], F32, name="z")
+            for j in range(4):
+                nc.tensor.matmul_mx(out=zq[:, j * P:(j + 1) * P], lhsT=w_perm[:, 1, j, :].bitcast(FP4X4),
+                                    lhsT_scale=ws_perm[:, 1, j, :], rhs=q_codes[:].bitcast(FP8X4), rhs_scale=q_scales[:],
+                                    start=True, stop=True)
+            nc.vector.tensor_tensor(out=bias[:], in0=zq[:].rearrange("p (j b) -> p j b", j=4),
+                                    in1=g1_t[:].unsqueeze(2).to_broadcast([P, 4, B]), op=ALU.add)
+
+        def finish_xg(b0, b1):
+            nc.vector.tensor_copy(out=xg[:, b0:b1, :], in_=acc[:, b0:b1, :])
+
+        prep(0)
+        state["prepped"] = 1
+        for item in production(0):
+            item()
+        relu(0)
+        next_piece = 0
+        while last_slot(next_piece) <= 0:
+            quantize(next_piece)
+            next_piece += 1
+        question()
+
+        produced = 0
+        relued = 0
+        early_te = early_ve = 0
+        for k in range(N_SLOTS):
+            target = min(k + LEAD, 1 + 2 * k, N_SLOTS - 1)
+            before = produced
+            todo = []
+            while produced < target:
+                produced += 1
+                todo = todo + production(produced)
+            relu_to = target - 1 if k >= LEAD and target < N_SLOTS - 1 else target
+            for j in range(4):
+                z_and_reduce(k, j)
+                for item in todo[len(todo) * j // 4:len(todo) * (j + 1) // 4]:
+                    item()
+                if j == 1:
+                    while next_piece < len(plan) and last_slot(next_piece) <= relued:
+                        quantize(next_piece)
+                        next_piece += 1
+                    while relued < before:
+                        relued += 1
+                        relu(relued)
+            while relued < relu_to:
+                relued += 1
+                relu(relued)
+            while (next_piece < len(plan) and last_slot(next_piece) <= relued
+                   and plan[next_piece][0] < (k + 2) * SLOT):
+                quantize(next_piece)
+                next_piece += 1
+            assert k + 1 >= N_SLOTS or next_piece == len(plan) or plan[next_piece][0] >= (k + 2) * SLOT
+            if k == N_SLOTS - 4:
+                early_te = sum(len(s) for kind, s in slots[0:k] if kind == "te")
+                early_ve = N_TE_SAMPLES + sum(len(s) for kind, s in slots[0:k] if kind == "ve")
+                finish_xg(0, early_te)
+                finish_xg(N_TE_SAMPLES, early_ve)
+
+        if early_te < N_TE_SAMPLES:
+            finish_xg(early_te, N_TE_SAMPLES)
+        finish_xg(early_ve, B)
+        nc.vector.quantize_mx(out=xg_codes[:].bitcast(FP8X4), scales=xg_scales[:], in_=xg[:].rearrange("p b t -> p (b t)"))
+        y = z_pool.tile([P, 512], F32, name="z")
+        nc.tensor.matmul_mx(out=y[:], lhsT=xg_codes[:].bitcast(FP8X4), lhsT_scale=xg_scales[:],
+                            rhs=f1_words[:].bitcast(FP4X4), rhs_scale=f1_scales[:], start=True, stop=True)
+        for c in (0, 1):
+            cols = slice(c * 256, (c + 1) * 256)
+            nc.vector.tensor_tensor(out=result[:, cols], in0=y[:, cols], in1=f1_bias[:, cols], op=ALU.add)
+            nc.scalar.activation(out=result[:, cols], in_=result[:, cols], func=ACT.Relu)
+            nc.sync.dma_start(out=out[:, cols], in_=result[:, cols])

@@ -30,10 +30,10 @@ PER_TILE = 9
 N_TILES = 9
 LEAD = 4
 SHIFTED = K - 3
-G_COUNT = (2, 4, 4, 4, 4, 4, 4, 4, 2)
-G_SPLIT = 3
-VEC_BANKS = [(k, 3) for k in range(4, 40) if k % 3 == 1] + [(41, 3), (42, 1), (42, 3)]
-LOAD_RUNS = ((0, 3), (3, 9), (9, 18), (18, 33), (33, 51))
+VEC_BANKS = [(42, 1), (42, 3)]
+SCALAR_UNITS = []
+TE_RING = 18
+TE_RUN = 6
 
 
 def slot_plan():
@@ -43,10 +43,10 @@ def slot_plan():
     while b < B:
         ve.append(("ve", list(range(b, min(b + PER_SLOT, B)))))
         b += PER_SLOT
-    order = [ve[0], te[0], te[1]]
-    n_te, n_ve = 2, 1
+    order = [ve[0], ve[1], te[0]]
+    n_te, n_ve = 1, 2
     while n_te + n_ve < N_SLOTS:
-        if n_te < N_TE and (n_te - 2) * len(ve) < n_ve * (N_TE - 2):
+        if n_te < N_TE and n_te * len(ve) < n_ve * N_TE:
             order.append(te[n_te])
             n_te += 1
         else:
@@ -79,7 +79,7 @@ def tile_rn_pa_w4_kernel(tc, u_i, u_j, g0_b, qst_bytes, qst_scale, g1_w_words, g
         ui_rows = u_i.rearrange("b d k -> (b d) k")
         uj_rows = u_j.rearrange("b d k -> (b d) k")
 
-        te_rows = keep.tile([P, N_TE_SAMPLES, K], BF16, align_bytes=64)
+        te_rows = keep.tile([P, TE_RING, K], BF16, align_bytes=64)
         ve_i = keep.tile([P, N_TILES, K], BF16, align_bytes=64)
         ve_j = keep.tile([P, N_TILES, K], BF16, align_bytes=64)
         g0_t = keep.tile([P, 4], BF16, align_bytes=64)
@@ -88,8 +88,8 @@ def tile_rn_pa_w4_kernel(tc, u_i, u_j, g0_b, qst_bytes, qst_scale, g1_w_words, g
         q_scale = keep.tile([P, K], F32, align_bytes=64)
         w_raw = keep.tile([P, 2, 1024], U8, align_bytes=64)
         ws_raw = keep.tile([P, 2, K], U8, align_bytes=64)
-        w_perm = keep.tile([P, 2, 4, 256], U8, align_bytes=64)
-        ws_perm = keep.tile([P, 2, 4, P], U8, align_bytes=64)
+        w_perm = keep.tile([P, 4, 256], U8, align_bytes=64)
+        ws_perm = keep.tile([P, 4, P], U8, align_bytes=64)
         f1_words = keep.tile([P, 1024], U8, align_bytes=64)
         f1_scales = keep.tile([P, K], U8, align_bytes=64)
         f1_bias = keep.tile([P, K], BF16, align_bytes=64)
@@ -101,7 +101,6 @@ def tile_rn_pa_w4_kernel(tc, u_i, u_j, g0_b, qst_bytes, qst_scale, g1_w_words, g
         codes = keep.tile([P, 2 * BLOCK], U32, align_bytes=64)
         scales = keep.tile([P, 2 * BLOCK], U8, align_bytes=64)
         ujg = keep.tile([P, 2, PER_TILE * D, 4], F32, align_bytes=64)
-        uis = keep.tile([P, 2, PER_TILE * D, 4], BF16, align_bytes=64)
         bias = keep.tile([P, 4, B], F32, align_bytes=64)
         acc = keep.tile([P, B, 4], F32, align_bytes=64)
         xg = keep.tile([P, B, 4], BF16, align_bytes=64)
@@ -109,24 +108,28 @@ def tile_rn_pa_w4_kernel(tc, u_i, u_j, g0_b, qst_bytes, qst_scale, g1_w_words, g
         xg_scales = keep.tile([P, B], U8, align_bytes=64)
         result = keep.tile([P, K], F32, align_bytes=64)
         q_val = keep.tile([P, K], BF16, align_bytes=64)
+        q_prod = keep.tile([P, K], F32, align_bytes=64)
         q_int = keep.tile([P, K], BF16, align_bytes=64)
         q_codes = keep.tile([P, B], U32, align_bytes=64)
         q_scales = keep.tile([P, B], U8, align_bytes=64)
         warm = keep.tile([P, 1], F32)
 
         nc.vector.memset(ws_raw[:].rearrange("p g n -> p (g n)").bitcast(I32), 0)
-        nc.vector.memset(f1_scales[:].bitcast(I32), 0)
         make_identity(nc, ident[:])
+        unused = te_rows[8 * D:P, :, :].rearrange("p s k -> p (s k)").bitcast(I32)
+        cut = 9 * K // 2
+        nc.vector.memset(unused[:, 0:cut], 0)
+        nc.gpsimd.memset(unused[:, cut:], 0)
+        nc.gpsimd.memset(f1_scales[:].bitcast(I32), 0)
 
         def load_te(s0, s1, queues):
+            n = s1 - s0
+            r0 = s0 % TE_RING
             for t in range(4):
-                queues[t % len(queues)].dma_start(
-                    out=te_rows[32 * t:32 * t + D, s0:s1, 0:SHIFTED],
-                    in_=ui_rows[D * s0:D * s1, t:t + SHIFTED].rearrange("(s r) k -> r s k", r=D))
-                for (p0, n, shift) in ((D, D, 0), (2 * D, 7, 1)):
-                    src = uj_rows[D * (s0 + shift):D * (s1 + shift), t:t + SHIFTED].rearrange("(s r) k -> r s k", r=D)
-                    queues[t % len(queues)].dma_start(out=te_rows[32 * t + p0:32 * t + p0 + n, s0:s1, 0:SHIFTED],
-                                                      in_=src[0:n])
+                for (p0, rows) in ((0, ui_rows), (4 * D, uj_rows)):
+                    queues[t % len(queues)].dma_start(
+                        out=te_rows[p0 + t:p0 + 4 * D:4, r0:r0 + n, 0:SHIFTED],
+                        in_=rows[D * s0:D * s1, t:t + SHIFTED].rearrange("(s r) k -> r s k", r=D))
 
         def ve_row0(v):
             return min((N_TE_SAMPLES + PER_TILE * v) * D, B * D - P)
@@ -139,31 +142,28 @@ def tile_rn_pa_w4_kernel(tc, u_i, u_j, g0_b, qst_bytes, qst_scale, g1_w_words, g
         def load_g0(s0, s1):
             for t in range(4):
                 nc.sync.dma_start(
-                    out=te_rows[32 * t + 31:32 * t + 32, s0:s1, 0:SHIFTED],
+                    out=te_rows[8 * D + t:8 * D + t + 1, s0:s1, 0:SHIFTED],
                     in_=g0_b[t:t + SHIFTED].partition_broadcast(1).unsqueeze(1).to_broadcast([1, s1 - s0, SHIFTED]))
 
         load_ve(0, nc.scalar)
-        nc.scalar.dma_start(out=g0_t[:], in_=g0_b.rearrange("(p t) -> p t", t=4))
+        nc.sync.dma_start(out=q_raw[:], in_=qst_bytes)
+        nc.sync.dma_start(out=q_scale[:], in_=qst_scale.rearrange("o k -> (o k)").partition_broadcast(P))
+        nc.sync.dma_start(out=g0_t[:], in_=g0_b.rearrange("(p t) -> p t", t=4))
+        nc.sync.dma_start(out=w_raw[:].bitcast(I32), in_=g1_w_words.rearrange("g p n -> p g n").bitcast(I32))
         for q in range(4):
             nc.sync.dma_start(out=ws_raw[32 * q:32 * q + 4, :, :].bitcast(I32),
                               in_=g1_w_scales[:, 4 * q:4 * q + 4, :].rearrange("g r n -> r g n").bitcast(I32))
-        nc.sync.dma_start(out=w_raw[:].bitcast(I32), in_=g1_w_words.rearrange("g p n -> p g n").bitcast(I32))
-        load_te(LOAD_RUNS[0][0], LOAD_RUNS[0][1], [nc.scalar, nc.sync])
-        load_g0(LOAD_RUNS[0][0], LOAD_RUNS[0][1])
-        nc.sync.dma_start(out=q_raw[:], in_=qst_bytes)
-        nc.sync.dma_start(out=q_scale[:], in_=qst_scale.rearrange("o k -> (o k)").partition_broadcast(P))
+        nc.scalar.activation(out=warm[:], in_=ident[:, 0:1], func=ACT.Relu)
         nc.sync.dma_start(out=g1_t[:], in_=g1_b.rearrange("(p t) -> p t", t=4))
-        load_te(LOAD_RUNS[1][0], LOAD_RUNS[1][1], [nc.sync])
-        load_g0(LOAD_RUNS[1][0], N_TE_SAMPLES)
+        load_te(0, 6, [nc.scalar, nc.sync])
+        load_g0(0, TE_RING)
         load_ve(1, nc.sync)
-        load_te(LOAD_RUNS[2][0], LOAD_RUNS[2][1], [nc.sync])
         load_ve(2, nc.sync)
-        load_ve(3, nc.sync)
-        load_te(LOAD_RUNS[3][0], LOAD_RUNS[3][1], [nc.sync])
-        load_ve(4, nc.sync)
-        load_ve(5, nc.sync)
-        load_te(LOAD_RUNS[4][0], LOAD_RUNS[4][1], [nc.sync])
-        for v in range(6, N_TILES):
+        load_te(6, 12, [nc.sync])
+        for v in range(3, 5):
+            load_ve(v, nc.sync)
+        load_te(12, 18, [nc.sync])
+        for v in range(5, N_TILES):
             load_ve(v, nc.sync)
         for q in range(4):
             nc.sync.dma_start(out=f1_scales[32 * q:32 * q + 4, :].bitcast(I32),
@@ -171,23 +171,21 @@ def tile_rn_pa_w4_kernel(tc, u_i, u_j, g0_b, qst_bytes, qst_scale, g1_w_words, g
         nc.sync.dma_start(out=f1_words[:].bitcast(I32), in_=f1_w_words[0].bitcast(I32))
         nc.sync.dma_start(out=f1_bias[:], in_=f1_b.partition_broadcast(P))
 
-        nc.scalar.activation(out=warm[:], in_=ident[:, 0:1], func=ACT.Relu)
-        nc.vector.tensor_copy(out=ident_bf[:], in_=ident[:])
-        by_t = ident_bf[:].rearrange("p (t r) -> p r t", t=4)
-        sel4 = sel[:].rearrange("p (a c) t -> p a c t", a=D)
-        nc.vector.tensor_tensor(out=sel4, in0=by_t[:, 0:D, :].unsqueeze(1).to_broadcast([P, D, D, 4]),
-                                in1=by_t[:, D:2 * D, :].unsqueeze(2).to_broadcast([P, D, D, 4]), op=ALU.add)
-        nc.vector.tensor_tensor(out=sel[:], in0=sel[:], in1=by_t[:, 31, :].unsqueeze(1).to_broadcast([P, PAIRS, 4]), op=ALU.add)
-        nc.vector.memset(zeros[:], 0.0)
         nc.vector.memset(h[:].rearrange("p (s n) t -> p s (n t)", n=SLOT)[:, :, PER_SLOT * PAIRS * 4:], 0.0)
 
-        def permute(engine, g):
-            nc.vector.tensor_copy(out=ws_perm[:, g], in_=ws_raw[:, g].rearrange("p (m j) -> p j m", j=4))
-            engine.tensor_copy(out=w_perm[:, g].rearrange("p j (m e) -> p j m e", e=2),
-                               in_=w_raw[:, g].rearrange("p (m j e) -> p j m e", j=4, e=2))
+        for j in range(4):
+            nc.gpsimd.tensor_copy(out=w_perm[:, j, :].rearrange("p (m e) -> p m e", e=2),
+                                  in_=w_raw[:, 0].rearrange("p (m j e) -> p j m e", j=4, e=2)[:, j])
 
-        permute(nc.vector, 0)
-        permute(nc.gpsimd, 1)
+        def make_sel():
+            nc.vector.tensor_copy(out=ident_bf[:], in_=ident[:])
+            by_t = ident_bf[:].rearrange("p (r t) -> p r t", t=4)
+            nc.vector.tensor_tensor(out=sel[:].rearrange("p (a c) t -> p a c t", a=D),
+                                    in0=by_t[:, 0:D, :].unsqueeze(1).to_broadcast([P, D, D, 4]),
+                                    in1=by_t[:, D:2 * D, :].unsqueeze(2).to_broadcast([P, D, D, 4]), op=ALU.add)
+            nc.vector.memset(zeros[:], 0.0)
+            nc.vector.tensor_tensor(out=sel[:], in0=sel[:], in1=by_t[:, 2 * D, :].unsqueeze(1).to_broadcast([P, PAIRS, 4]),
+                                    op=ALU.add)
 
         slots = slot_plan()
         assert len(slots) == N_SLOTS
@@ -206,19 +204,6 @@ def tile_rn_pa_w4_kernel(tc, u_i, u_j, g0_b, qst_bytes, qst_scale, g1_w_words, g
             b0 = N_TE_SAMPLES + PER_TILE * v
             return list(range(b0, min(b0 + PER_TILE, B)))
 
-        def on_gpsimd(b):
-            v = (b - N_TE_SAMPLES) // PER_TILE
-            samples = tile_samples(v)
-            return b >= samples[-1] + 1 - G_COUNT[v]
-
-        def sum_pairs(engine, b, a0, a1, u_i_rows, u_j_rows):
-            n = a1 - a0
-            lo = slot_of[b]
-            engine.tensor_tensor(
-                out=h[:, lo + a0 * D:lo + a1 * D, :].rearrange("p (a c) t -> p a c t", a=n),
-                in0=u_i_rows.unsqueeze(1).to_broadcast([P, n, D, 4]),
-                in1=u_j_rows[:, a0:a1, :].unsqueeze(2).to_broadcast([P, n, D, 4]), op=ALU.add)
-
         def prep(v):
             xt = xt_pool.tile([P, 2, P, 2], F32, name="xt")
             xts[v] = xt
@@ -233,16 +218,6 @@ def tile_rn_pa_w4_kernel(tc, u_i, u_j, g0_b, qst_bytes, qst_scale, g1_w_words, g
                 out=ujg[:, v % 2, 0:n, :],
                 in0=xt[:, 1, off:off + n, :].rearrange("p r u -> p (r u)").bitcast(BF16).rearrange("p (r t) -> p r t", t=4),
                 in1=g0_t[:].unsqueeze(1).to_broadcast([P, n, 4]), op=ALU.add)
-            n_g = G_COUNT[v] * D
-            if n_g:
-                nc.vector.tensor_copy(out=uis[:, v % 2, n - n_g:n, :].rearrange("p r t -> p (r t)").bitcast(F32),
-                                      in_=xt[:, 0, off + n - n_g:off + n, :].rearrange("p r u -> p (r u)"))
-                for i, b in enumerate(samples):
-                    if on_gpsimd(b):
-                        for a in range(0, D, D // G_SPLIT):
-                            sum_pairs(nc.gpsimd, b, a, a + D // G_SPLIT, uis[:, v % 2, i * D:(i + 1) * D, :],
-                                      ujg[:, v % 2, i * D:(i + 1) * D, :])
-
         state = {"prepped": 0}
 
         def te_unit(k, unit, samples):
@@ -251,26 +226,31 @@ def tile_rn_pa_w4_kernel(tc, u_i, u_j, g0_b, qst_bytes, qst_scale, g1_w_words, g
                 half = 3 * unit + r
                 b = samples[half // 2]
                 nc.tensor.matmul(ph[:, 288 * r:288 * (r + 1)],
-                                 lhsT=te_rows[:, b, :].rearrange("p (m t) -> p t m", t=4)[:, 0, :],
+                                 lhsT=te_rows[:, b % TE_RING, :].rearrange("p (m t) -> p t m", t=4)[:, 0, :],
                                  rhs=sel[:, 72 * (half % 2):72 * (half % 2) + 72, :].rearrange("p n t -> p (n t)"),
                                  start=True, stop=True)
             lo = column(k) + 216 * unit
             dst = h[:, lo:lo + 216, :].rearrange("p n t -> p (n t)")
-            if k < 4 and unit == 1:
+            if (k, unit) in SCALAR_UNITS:
                 nc.scalar.activation(out=dst, in_=ph[:, 0:864], func=ACT.Relu)
             else:
                 nc.vector.tensor_scalar_max(dst, ph[:, 0:864], 0.0)
 
-        def ve_sample(b):
-            v = (b - N_TE_SAMPLES) // PER_TILE
-            if (b - N_TE_SAMPLES) % PER_TILE == 3 and state["prepped"] == v + 1 and v + 1 < N_TILES:
+        def ve_sums(k, samples):
+            b = samples[0]
+            n = len(samples)
+            v, i = divmod(b - N_TE_SAMPLES, PER_TILE)
+            if i == 2 * PER_SLOT and state["prepped"] == v + 1 and v + 1 < N_TILES:
                 prep(v + 1)
                 state["prepped"] = v + 2
-            if not on_gpsimd(b):
-                off = b * D - ve_row0(v)
-                ui_bf = xts[v][:, 0, off:off + D, :].rearrange("p r u -> p (r u)").bitcast(BF16)
-                i = (b - N_TE_SAMPLES) % PER_TILE
-                sum_pairs(nc.vector, b, 0, D, ui_bf.rearrange("p (c t) -> p c t", t=4), ujg[:, v % 2, i * D:(i + 1) * D, :])
+            off = b * D - ve_row0(v)
+            ui_bf = xts[v][:, 0, off:off + n * D, :].rearrange("p r u -> p (r u)").bitcast(BF16)
+            nc.vector.tensor_tensor(
+                out=h[:, column(k):column(k) + n * PAIRS, :].rearrange("p (s a c) t -> p s a c t", s=n, a=D),
+                in0=ui_bf.rearrange("p (s c t) -> p s c t", c=D, t=4).unsqueeze(2).to_broadcast([P, n, D, D, 4]),
+                in1=ujg[:, v % 2, i * D:(i + n) * D, :].rearrange("p (s a) t -> p s a t", a=D).unsqueeze(3).to_broadcast(
+                    [P, n, D, D, 4]),
+                op=ALU.add)
 
         def relu(k):
             if slots[k][0] == "ve":
@@ -281,8 +261,10 @@ def tile_rn_pa_w4_kernel(tc, u_i, u_j, g0_b, qst_bytes, qst_scale, g1_w_words, g
         def production(k):
             kind, samples = slots[k]
             if kind == "te":
-                return [lambda k=k, unit=unit, samples=samples: te_unit(k, unit, samples) for unit in (0, 1)]
-            return [lambda b=b: ve_sample(b) for b in samples]
+                return [lambda k=k, unit=unit, samples=samples: te_unit(k, unit, samples) for unit in (0, 1)] + (
+                    [lambda b=samples[-1] + 1: load_te(b - TE_RUN + TE_RING, min(b + TE_RING, N_TE_SAMPLES), [nc.sync])]
+                    if (samples[-1] + 1) % TE_RUN == 0 and samples[-1] + 1 - TE_RUN + TE_RING < N_TE_SAMPLES else [])
+            return [lambda k=k, samples=samples: ve_sums(k, samples)]
 
         plan = quantize_plan()
 
@@ -302,7 +284,7 @@ def tile_rn_pa_w4_kernel(tc, u_i, u_j, g0_b, qst_bytes, qst_scale, g1_w_words, g
             second = 192 if len(samples) == PER_SLOT else 64
             for w in (0, second):
                 lo = column(k) + w
-                nc.tensor.matmul_mx(out=z[:, w:w + 256], lhsT=w_perm[:, 0, j, :].bitcast(FP4X4), lhsT_scale=ws_perm[:, 0, j, :],
+                nc.tensor.matmul_mx(out=z[:, w:w + 256], lhsT=w_perm[:, j, :].bitcast(FP4X4), lhsT_scale=ws_perm[:, j, :],
                                     rhs=codes[:, lo:lo + 256].bitcast(FP8X4), rhs_scale=scales[:, lo:lo + 256],
                                     start=True, stop=True)
             for s, b in enumerate(samples):
@@ -315,27 +297,37 @@ def tile_rn_pa_w4_kernel(tc, u_i, u_j, g0_b, qst_bytes, qst_scale, g1_w_words, g
                     nc.scalar.activation(out=junk[:], in_=src, func=ACT.Relu, bias=bias[:, j, b:b + 1],
                                          accum_out=acc[:, b, j:j + 1])
 
-        def question():
+        def question_values():
             nc.vector.tensor_tensor(out=q_val[:], in0=q_raw[:].bitcast(FP8), in1=q_scale[:], op=ALU.mult)
+
+        def question_turn():
             xq = xt_pool.tile([P, 2, P, 2], F32, name="xt")
             words = q_val[:].bitcast(F32)
             for u in (0, 1):
                 nc.tensor.transpose(xq[:, 0, :, u], words[:, u:K // 2:2], ident[:])
-            nc.vector.tensor_copy(out=q_int[:].bitcast(F32), in_=xq[:, 0].rearrange("p r u -> p (r u)"))
+            nc.scalar.copy(out=q_int[:].bitcast(F32), in_=xq[:, 0].rearrange("p r u -> p (r u)"))
+
+        def question_product():
             nc.vector.quantize_mx(out=q_codes[:].bitcast(FP8X4), scales=q_scales[:], in_=q_int[:])
             zq = z_pool.tile([P, 512], F32, name="z")
+            nc.tensor.matmul_mx(out=zq[:], lhsT=q_codes[:].bitcast(FP8X4), lhsT_scale=q_scales[:],
+                                rhs=w_raw[:, 1, :].bitcast(FP4X4), rhs_scale=ws_raw[:, 1, :], start=True, stop=True)
+            nc.scalar.copy(out=q_prod[:], in_=zq[:])
+            zqt = z_pool.tile([P, 512], F32, name="z")
             for j in range(4):
-                nc.tensor.matmul_mx(out=zq[:, j * P:(j + 1) * P], lhsT=w_perm[:, 1, j, :].bitcast(FP4X4),
-                                    lhsT_scale=ws_perm[:, 1, j, :], rhs=q_codes[:].bitcast(FP8X4), rhs_scale=q_scales[:],
-                                    start=True, stop=True)
-            nc.vector.tensor_tensor(out=bias[:], in0=zq[:].rearrange("p (j b) -> p j b", j=4),
-                                    in1=g1_t[:].unsqueeze(2).to_broadcast([P, 4, B]), op=ALU.add)
+                nc.tensor.transpose(zqt[:, j * P:(j + 1) * P], q_prod[:].rearrange("p (m j) -> p j m", j=4)[:, j, :], ident[:])
+            for j in range(4):
+                nc.scalar.activation(out=bias[:, j, :], in_=zqt[:, j * P:(j + 1) * P], func=ACT.Identity, bias=g1_t[:, j:j + 1])
 
         def finish_xg(b0, b1):
             nc.vector.tensor_copy(out=xg[:, b0:b1, :], in_=acc[:, b0:b1, :])
 
+        question_values()
+        question_turn()
         prep(0)
         state["prepped"] = 1
+        question_product()
+        nc.vector.tensor_copy(out=ws_perm[:], in_=ws_raw[:, 0].rearrange("p (m j) -> p j m", j=4))
         for item in production(0):
             item()
         relu(0)
@@ -343,7 +335,7 @@ def tile_rn_pa_w4_kernel(tc, u_i, u_j, g0_b, qst_bytes, qst_scale, g1_w_words, g
         while last_slot(next_piece) <= 0:
             quantize(next_piece)
             next_piece += 1
-        question()
+        make_sel()
 
         produced = 0
         relued = 0

@@ -29,11 +29,11 @@ N_TE_SAMPLES = N_TE * PER_SLOT
 PER_TILE = 9
 N_TILES = 9
 LEAD = 4
+HEAD_VE = 12
 SHIFTED = K - 3
-VEC_BANKS = [(42, 1), (42, 3)]
+VEC_BANKS = [(k, 3) for k in range(8, 41) if k % 9 == 1] + [(41, 3), (42, 1), (42, 3)]
 SCALAR_UNITS = []
-TE_RING = 18
-TE_RUN = 6
+TE_RUNS = ((0, 6), (6, 18), (18, N_TE_SAMPLES))
 
 
 def slot_plan():
@@ -43,10 +43,10 @@ def slot_plan():
     while b < B:
         ve.append(("ve", list(range(b, min(b + PER_SLOT, B)))))
         b += PER_SLOT
-    order = [ve[0], ve[1], te[0]]
-    n_te, n_ve = 1, 2
+    order = ve[0:HEAD_VE]
+    n_te, n_ve = 0, HEAD_VE
     while n_te + n_ve < N_SLOTS:
-        if n_te < N_TE and n_te * len(ve) < n_ve * N_TE:
+        if n_te < N_TE and n_te * (len(ve) - HEAD_VE) < (n_ve - HEAD_VE + 1) * N_TE - N_TE // 2:
             order.append(te[n_te])
             n_te += 1
         else:
@@ -79,7 +79,7 @@ def tile_rn_pa_w4_kernel(tc, u_i, u_j, g0_b, qst_bytes, qst_scale, g1_w_words, g
         ui_rows = u_i.rearrange("b d k -> (b d) k")
         uj_rows = u_j.rearrange("b d k -> (b d) k")
 
-        te_rows = keep.tile([P, TE_RING, K], BF16, align_bytes=64)
+        te_rows = keep.tile([P, N_TE_SAMPLES, K], BF16, align_bytes=64)
         ve_i = keep.tile([P, N_TILES, K], BF16, align_bytes=64)
         ve_j = keep.tile([P, N_TILES, K], BF16, align_bytes=64)
         g0_t = keep.tile([P, 4], BF16, align_bytes=64)
@@ -116,19 +116,20 @@ def tile_rn_pa_w4_kernel(tc, u_i, u_j, g0_b, qst_bytes, qst_scale, g1_w_words, g
 
         nc.vector.memset(ws_raw[:].rearrange("p g n -> p (g n)").bitcast(I32), 0)
         make_identity(nc, ident[:])
-        unused = te_rows[8 * D:P, :, :].rearrange("p s k -> p (s k)").bitcast(I32)
-        cut = 9 * K // 2
-        nc.vector.memset(unused[:, 0:cut], 0)
-        nc.gpsimd.memset(unused[:, cut:], 0)
+        spare = te_rows[8 * D:P, :, :].rearrange("p s k -> p (s k)").bitcast(I32)
+
+        def clear_spare(engine, s0, s1):
+            engine.memset(spare[:, s0 * K // 2:s1 * K // 2], 0)
+
+        clear_spare(nc.vector, *TE_RUNS[0])
+        clear_spare(nc.gpsimd, *TE_RUNS[1])
         nc.gpsimd.memset(f1_scales[:].bitcast(I32), 0)
 
         def load_te(s0, s1, queues):
-            n = s1 - s0
-            r0 = s0 % TE_RING
             for t in range(4):
                 for (p0, rows) in ((0, ui_rows), (4 * D, uj_rows)):
                     queues[t % len(queues)].dma_start(
-                        out=te_rows[p0 + t:p0 + 4 * D:4, r0:r0 + n, 0:SHIFTED],
+                        out=te_rows[p0 + t:p0 + 4 * D:4, s0:s1, 0:SHIFTED],
                         in_=rows[D * s0:D * s1, t:t + SHIFTED].rearrange("(s r) k -> r s k", r=D))
 
         def ve_row0(v):
@@ -155,14 +156,20 @@ def tile_rn_pa_w4_kernel(tc, u_i, u_j, g0_b, qst_bytes, qst_scale, g1_w_words, g
                               in_=g1_w_scales[:, 4 * q:4 * q + 4, :].rearrange("g r n -> r g n").bitcast(I32))
         nc.scalar.activation(out=warm[:], in_=ident[:, 0:1], func=ACT.Relu)
         nc.sync.dma_start(out=g1_t[:], in_=g1_b.rearrange("(p t) -> p t", t=4))
-        load_te(0, 6, [nc.scalar, nc.sync])
-        load_g0(0, TE_RING)
+        for j in range(4):
+            nc.gpsimd.tensor_copy(out=w_perm[:, j, :].rearrange("p (m e) -> p m e", e=2),
+                                  in_=w_raw[:, 0].rearrange("p (m j e) -> p j m e", j=4, e=2)[:, j])
+        clear_spare(nc.gpsimd, *TE_RUNS[2])
         load_ve(1, nc.sync)
+        load_te(*TE_RUNS[0], [nc.sync])
+        load_g0(*TE_RUNS[0])
         load_ve(2, nc.sync)
-        load_te(6, 12, [nc.sync])
-        for v in range(3, 5):
-            load_ve(v, nc.sync)
-        load_te(12, 18, [nc.sync])
+        load_te(*TE_RUNS[1], [nc.sync])
+        load_g0(*TE_RUNS[1])
+        load_ve(3, nc.sync)
+        load_ve(4, nc.sync)
+        load_te(*TE_RUNS[2], [nc.sync])
+        load_g0(*TE_RUNS[2])
         for v in range(5, N_TILES):
             load_ve(v, nc.sync)
         for q in range(4):
@@ -172,10 +179,6 @@ def tile_rn_pa_w4_kernel(tc, u_i, u_j, g0_b, qst_bytes, qst_scale, g1_w_words, g
         nc.sync.dma_start(out=f1_bias[:], in_=f1_b.partition_broadcast(P))
 
         nc.vector.memset(h[:].rearrange("p (s n) t -> p s (n t)", n=SLOT)[:, :, PER_SLOT * PAIRS * 4:], 0.0)
-
-        for j in range(4):
-            nc.gpsimd.tensor_copy(out=w_perm[:, j, :].rearrange("p (m e) -> p m e", e=2),
-                                  in_=w_raw[:, 0].rearrange("p (m j e) -> p j m e", j=4, e=2)[:, j])
 
         def make_sel():
             nc.vector.tensor_copy(out=ident_bf[:], in_=ident[:])
@@ -204,31 +207,38 @@ def tile_rn_pa_w4_kernel(tc, u_i, u_j, g0_b, qst_bytes, qst_scale, g1_w_words, g
             b0 = N_TE_SAMPLES + PER_TILE * v
             return list(range(b0, min(b0 + PER_TILE, B)))
 
-        def prep(v):
+        def turn_rows(v):
             xt = xt_pool.tile([P, 2, P, 2], F32, name="xt")
             xts[v] = xt
             for i, src in ((1, ve_j), (0, ve_i)):
                 words = src[:, v, :].bitcast(F32)
                 for u in (0, 1):
                     nc.tensor.transpose(xt[:, i, :, u], words[:, u:K // 2:2], ident[:])
+
+        def add_bias(v):
             samples = tile_samples(v)
             off = samples[0] * D - ve_row0(v)
             n = len(samples) * D
             nc.vector.tensor_tensor(
                 out=ujg[:, v % 2, 0:n, :],
-                in0=xt[:, 1, off:off + n, :].rearrange("p r u -> p (r u)").bitcast(BF16).rearrange("p (r t) -> p r t", t=4),
+                in0=xts[v][:, 1, off:off + n, :].rearrange("p r u -> p (r u)").bitcast(BF16).rearrange("p (r t) -> p r t", t=4),
                 in1=g0_t[:].unsqueeze(1).to_broadcast([P, n, 4]), op=ALU.add)
-        state = {"prepped": 0}
 
-        def te_unit(k, unit, samples):
+        phs = {}
+
+        def te_products(k, unit, samples):
             ph = ph_pool.tile([P, 1024], BF16, name="ph")
+            phs[(k, unit)] = ph
             for r in range(3):
                 half = 3 * unit + r
                 b = samples[half // 2]
                 nc.tensor.matmul(ph[:, 288 * r:288 * (r + 1)],
-                                 lhsT=te_rows[:, b % TE_RING, :].rearrange("p (m t) -> p t m", t=4)[:, 0, :],
+                                 lhsT=te_rows[:, b, :].rearrange("p (m t) -> p t m", t=4)[:, 0, :],
                                  rhs=sel[:, 72 * (half % 2):72 * (half % 2) + 72, :].rearrange("p n t -> p (n t)"),
                                  start=True, stop=True)
+
+        def te_relu(k, unit):
+            ph = phs.pop((k, unit))
             lo = column(k) + 216 * unit
             dst = h[:, lo:lo + 216, :].rearrange("p n t -> p (n t)")
             if (k, unit) in SCALAR_UNITS:
@@ -236,13 +246,17 @@ def tile_rn_pa_w4_kernel(tc, u_i, u_j, g0_b, qst_bytes, qst_scale, g1_w_words, g
             else:
                 nc.vector.tensor_scalar_max(dst, ph[:, 0:864], 0.0)
 
+        def ve_tensor(samples):
+            v, i = divmod(samples[0] - N_TE_SAMPLES, PER_TILE)
+            if i == 2 * PER_SLOT and v + 1 < N_TILES:
+                turn_rows(v + 1)
+
         def ve_sums(k, samples):
             b = samples[0]
             n = len(samples)
             v, i = divmod(b - N_TE_SAMPLES, PER_TILE)
-            if i == 2 * PER_SLOT and state["prepped"] == v + 1 and v + 1 < N_TILES:
-                prep(v + 1)
-                state["prepped"] = v + 2
+            if i == 0 and v > 0:
+                add_bias(v)
             off = b * D - ve_row0(v)
             ui_bf = xts[v][:, 0, off:off + n * D, :].rearrange("p r u -> p (r u)").bitcast(BF16)
             nc.vector.tensor_tensor(
@@ -258,13 +272,21 @@ def tile_rn_pa_w4_kernel(tc, u_i, u_j, g0_b, qst_bytes, qst_scale, g1_w_words, g
                 flat = h[:, column(k):column(k) + n, :].rearrange("p n t -> p (n t)")
                 nc.vector.tensor_scalar_max(flat, flat, 0.0)
 
-        def production(k):
-            kind, samples = slots[k]
+        items = []
+        for k, (kind, samples) in enumerate(slots):
             if kind == "te":
-                return [lambda k=k, unit=unit, samples=samples: te_unit(k, unit, samples) for unit in (0, 1)] + (
-                    [lambda b=samples[-1] + 1: load_te(b - TE_RUN + TE_RING, min(b + TE_RING, N_TE_SAMPLES), [nc.sync])]
-                    if (samples[-1] + 1) % TE_RUN == 0 and samples[-1] + 1 - TE_RUN + TE_RING < N_TE_SAMPLES else [])
-            return [lambda k=k, samples=samples: ve_sums(k, samples)]
+                for unit in (0, 1):
+                    items.append((k, lambda k=k, unit=unit, samples=samples: te_products(k, unit, samples),
+                                  lambda k=k, unit=unit: te_relu(k, unit)))
+            else:
+                items.append((k, lambda samples=samples: ve_tensor(samples), lambda k=k, samples=samples: ve_sums(k, samples)))
+        state = {"tensor": 0}
+
+        def produce(n):
+            while state["tensor"] < min(n + 2, len(items)):
+                items[state["tensor"]][1]()
+                state["tensor"] += 1
+            items[n][2]()
 
         plan = quantize_plan()
 
@@ -324,12 +346,11 @@ def tile_rn_pa_w4_kernel(tc, u_i, u_j, g0_b, qst_bytes, qst_scale, g1_w_words, g
 
         question_values()
         question_turn()
-        prep(0)
-        state["prepped"] = 1
+        turn_rows(0)
+        add_bias(0)
         question_product()
         nc.vector.tensor_copy(out=ws_perm[:], in_=ws_raw[:, 0].rearrange("p (m j) -> p j m", j=4))
-        for item in production(0):
-            item()
+        produce(0)
         relu(0)
         next_piece = 0
         while last_slot(next_piece) <= 0:
@@ -338,20 +359,23 @@ def tile_rn_pa_w4_kernel(tc, u_i, u_j, g0_b, qst_bytes, qst_scale, g1_w_words, g
         make_sel()
 
         produced = 0
+        next_item = 1
         relued = 0
         early_te = early_ve = 0
         for k in range(N_SLOTS):
             target = min(k + LEAD, 1 + 2 * k, N_SLOTS - 1)
             before = produced
-            todo = []
-            while produced < target:
-                produced += 1
-                todo = todo + production(produced)
+            produced = target
+            end = next_item
+            while end < len(items) and items[end][0] <= produced:
+                end += 1
+            todo = range(next_item, end)
+            next_item = end
             relu_to = target - 1 if k >= LEAD and target < N_SLOTS - 1 else target
             for j in range(4):
                 z_and_reduce(k, j)
-                for item in todo[len(todo) * j // 4:len(todo) * (j + 1) // 4]:
-                    item()
+                for n in todo[len(todo) * j // 4:len(todo) * (j + 1) // 4]:
+                    produce(n)
                 if j == 1:
                     while next_piece < len(plan) and last_slot(next_piece) <= relued:
                         quantize(next_piece)

@@ -29,11 +29,11 @@ N_TE_SAMPLES = N_TE * PER_SLOT
 PER_TILE = 9
 N_TILES = 9
 LEAD = 4
-HEAD_VE = 12
-SHIFTED = K - 3
-VEC_BANKS = [(k, 3) for k in range(8, 41) if k % 9 == 1] + [(41, 3), (42, 1), (42, 3)]
+RAMP = 0
+VEC_BANKS = [(k, 3) for k in range(8, 39) if k % 3 == 1] + [(39, 1), (39, 3), (40, 1), (40, 3), (41, 1), (41, 3), (42, 1), (42, 3)]
 SCALAR_UNITS = []
-TE_RUNS = ((0, 6), (6, 18), (18, N_TE_SAMPLES))
+N_TE_TILES = 6
+Z_BANKS = 3
 
 
 def slot_plan():
@@ -43,10 +43,10 @@ def slot_plan():
     while b < B:
         ve.append(("ve", list(range(b, min(b + PER_SLOT, B)))))
         b += PER_SLOT
-    order = ve[0:HEAD_VE]
-    n_te, n_ve = 0, HEAD_VE
+    order = []
+    n_te, n_ve = 0, 0
     while n_te + n_ve < N_SLOTS:
-        if n_te < N_TE and n_te * (len(ve) - HEAD_VE) < (n_ve - HEAD_VE + 1) * N_TE - N_TE // 2:
+        if n_te < N_TE and n_te * len(ve) <= n_ve * N_TE + 0:
             order.append(te[n_te])
             n_te += 1
         else:
@@ -56,7 +56,7 @@ def slot_plan():
 
 
 def quantize_plan():
-    widths = [256, 128, 64] * 2 + [512] * 5 + [128]
+    widths = [256, 128, 64] * 4 + [512] * 3 + [256]
     widths += [512] * (4 * 7) + [512, 512, 256]
     plan, at = [], 0
     for w in widths:
@@ -71,7 +71,8 @@ def tile_rn_pa_w4_kernel(tc, u_i, u_j, g0_b, qst_bytes, qst_scale, g1_w_words, g
     with ExitStack() as ctx:
         keep = ctx.enter_context(tc.tile_pool(name="keep", bufs=1))
         junk_pool = ctx.enter_context(tc.tile_pool(name="junk_pool", bufs=6))
-        z_pool = ctx.enter_context(tc.psum_pool(name="z_pool", bufs=4))
+        z_pool = ctx.enter_context(tc.psum_pool(name="z_pool", bufs=Z_BANKS))
+        tb_pool = ctx.enter_context(tc.psum_pool(name="tb_pool", bufs=1))
         ph_pool = ctx.enter_context(tc.psum_pool(name="ph_pool", bufs=2))
         xt_pool = ctx.enter_context(tc.psum_pool(name="xt_pool", bufs=2))
         ctx.enter_context(tc.manual_schedule())
@@ -79,7 +80,10 @@ def tile_rn_pa_w4_kernel(tc, u_i, u_j, g0_b, qst_bytes, qst_scale, g1_w_words, g
         ui_rows = u_i.rearrange("b d k -> (b d) k")
         uj_rows = u_j.rearrange("b d k -> (b d) k")
 
-        te_rows = keep.tile([P, N_TE_SAMPLES, K], BF16, align_bytes=64)
+        te_i = keep.tile([P, N_TE_TILES, K], BF16, align_bytes=64)
+        te_j = keep.tile([P, N_TE_TILES, K], BF16, align_bytes=64)
+        te_cols = keep.tile([P, 2, PER_TILE, 32, 4], BF16, align_bytes=64)
+        te_rows = keep.tile([P, 4, PER_SLOT, P], BF16, align_bytes=64)
         ve_i = keep.tile([P, N_TILES, K], BF16, align_bytes=64)
         ve_j = keep.tile([P, N_TILES, K], BF16, align_bytes=64)
         g0_t = keep.tile([P, 4], BF16, align_bytes=64)
@@ -116,21 +120,12 @@ def tile_rn_pa_w4_kernel(tc, u_i, u_j, g0_b, qst_bytes, qst_scale, g1_w_words, g
 
         nc.vector.memset(ws_raw[:].rearrange("p g n -> p (g n)").bitcast(I32), 0)
         make_identity(nc, ident[:])
-        spare = te_rows[8 * D:P, :, :].rearrange("p s k -> p (s k)").bitcast(I32)
-
-        def clear_spare(engine, s0, s1):
-            engine.memset(spare[:, s0 * K // 2:s1 * K // 2], 0)
-
-        clear_spare(nc.vector, *TE_RUNS[0])
-        clear_spare(nc.gpsimd, *TE_RUNS[1])
         nc.gpsimd.memset(f1_scales[:].bitcast(I32), 0)
 
-        def load_te(s0, s1, queues):
-            for t in range(4):
-                for (p0, rows) in ((0, ui_rows), (4 * D, uj_rows)):
-                    queues[t % len(queues)].dma_start(
-                        out=te_rows[p0 + t:p0 + 4 * D:4, s0:s1, 0:SHIFTED],
-                        in_=rows[D * s0:D * s1, t:t + SHIFTED].rearrange("(s r) k -> r s k", r=D))
+        def load_te(v, queue):
+            r0 = PER_TILE * D * v
+            queue.dma_start(out=te_i[:, v, :], in_=ui_rows[r0:r0 + P, :])
+            queue.dma_start(out=te_j[:, v, :], in_=uj_rows[r0:r0 + P, :])
 
         def ve_row0(v):
             return min((N_TE_SAMPLES + PER_TILE * v) * D, B * D - P)
@@ -140,37 +135,28 @@ def tile_rn_pa_w4_kernel(tc, u_i, u_j, g0_b, qst_bytes, qst_scale, g1_w_words, g
             queue.dma_start(out=ve_j[:, v, :], in_=uj_rows[r0:r0 + P, :])
             queue.dma_start(out=ve_i[:, v, :], in_=ui_rows[r0:r0 + P, :])
 
-        def load_g0(s0, s1):
-            for t in range(4):
-                nc.sync.dma_start(
-                    out=te_rows[8 * D + t:8 * D + t + 1, s0:s1, 0:SHIFTED],
-                    in_=g0_b[t:t + SHIFTED].partition_broadcast(1).unsqueeze(1).to_broadcast([1, s1 - s0, SHIFTED]))
-
-        load_ve(0, nc.scalar)
-        nc.sync.dma_start(out=q_raw[:], in_=qst_bytes)
-        nc.sync.dma_start(out=q_scale[:], in_=qst_scale.rearrange("o k -> (o k)").partition_broadcast(P))
+        load_te(0, nc.scalar)
         nc.sync.dma_start(out=g0_t[:], in_=g0_b.rearrange("(p t) -> p t", t=4))
         nc.sync.dma_start(out=w_raw[:].bitcast(I32), in_=g1_w_words.rearrange("g p n -> p g n").bitcast(I32))
+        nc.sync.dma_start(out=q_raw[:], in_=qst_bytes)
+        nc.sync.dma_start(out=q_scale[:], in_=qst_scale.rearrange("o k -> (o k)").partition_broadcast(P))
         for q in range(4):
             nc.sync.dma_start(out=ws_raw[32 * q:32 * q + 4, :, :].bitcast(I32),
                               in_=g1_w_scales[:, 4 * q:4 * q + 4, :].rearrange("g r n -> r g n").bitcast(I32))
         nc.scalar.activation(out=warm[:], in_=ident[:, 0:1], func=ACT.Relu)
+        load_ve(0, nc.sync)
         nc.sync.dma_start(out=g1_t[:], in_=g1_b.rearrange("(p t) -> p t", t=4))
-        for j in range(4):
-            nc.gpsimd.tensor_copy(out=w_perm[:, j, :].rearrange("p (m e) -> p m e", e=2),
-                                  in_=w_raw[:, 0].rearrange("p (m j e) -> p j m e", j=4, e=2)[:, j])
-        clear_spare(nc.gpsimd, *TE_RUNS[2])
         load_ve(1, nc.sync)
-        load_te(*TE_RUNS[0], [nc.sync])
-        load_g0(*TE_RUNS[0])
+        load_te(1, nc.sync)
         load_ve(2, nc.sync)
-        load_te(*TE_RUNS[1], [nc.sync])
-        load_g0(*TE_RUNS[1])
+        load_te(2, nc.sync)
         load_ve(3, nc.sync)
+        load_te(3, nc.sync)
         load_ve(4, nc.sync)
-        load_te(*TE_RUNS[2], [nc.sync])
-        load_g0(*TE_RUNS[2])
-        for v in range(5, N_TILES):
+        load_te(4, nc.sync)
+        load_ve(5, nc.sync)
+        load_te(5, nc.sync)
+        for v in range(6, N_TILES):
             load_ve(v, nc.sync)
         for q in range(4):
             nc.sync.dma_start(out=f1_scales[32 * q:32 * q + 4, :].bitcast(I32),
@@ -180,15 +166,15 @@ def tile_rn_pa_w4_kernel(tc, u_i, u_j, g0_b, qst_bytes, qst_scale, g1_w_words, g
 
         nc.vector.memset(h[:].rearrange("p (s n) t -> p s (n t)", n=SLOT)[:, :, PER_SLOT * PAIRS * 4:], 0.0)
 
-        def make_sel():
-            nc.vector.tensor_copy(out=ident_bf[:], in_=ident[:])
-            by_t = ident_bf[:].rearrange("p (r t) -> p r t", t=4)
-            nc.vector.tensor_tensor(out=sel[:].rearrange("p (a c) t -> p a c t", a=D),
-                                    in0=by_t[:, 0:D, :].unsqueeze(1).to_broadcast([P, D, D, 4]),
-                                    in1=by_t[:, D:2 * D, :].unsqueeze(2).to_broadcast([P, D, D, 4]), op=ALU.add)
-            nc.vector.memset(zeros[:], 0.0)
-            nc.vector.tensor_tensor(out=sel[:], in0=sel[:], in1=by_t[:, 2 * D, :].unsqueeze(1).to_broadcast([P, PAIRS, 4]),
-                                    op=ALU.add)
+        nc.vector.tensor_copy(out=ident_bf[:], in_=ident[:])
+        by_t = ident_bf[:].rearrange("p (r t) -> p r t", t=4)
+        nc.vector.memset(te_cols[:, :, :, 2 * D + 1:, :].rearrange("p v s r t -> p (v s) (r t)"), 0.0)
+        nc.vector.tensor_tensor(out=sel[:].rearrange("p (a c) t -> p a c t", a=D),
+                                in0=by_t[:, 0:D, :].unsqueeze(1).to_broadcast([P, D, D, 4]),
+                                in1=by_t[:, D:2 * D, :].unsqueeze(2).to_broadcast([P, D, D, 4]), op=ALU.add)
+        nc.vector.memset(zeros[:], 0.0)
+        nc.vector.tensor_tensor(out=sel[:], in0=sel[:], in1=by_t[:, 2 * D, :].unsqueeze(1).to_broadcast([P, PAIRS, 4]),
+                                op=ALU.add)
 
         slots = slot_plan()
         assert len(slots) == N_SLOTS
@@ -224,6 +210,31 @@ def tile_rn_pa_w4_kernel(tc, u_i, u_j, g0_b, qst_bytes, qst_scale, g1_w_words, g
                 in0=xts[v][:, 1, off:off + n, :].rearrange("p r u -> p (r u)").bitcast(BF16).rearrange("p (r t) -> p r t", t=4),
                 in1=g0_t[:].unsqueeze(1).to_broadcast([P, n, 4]), op=ALU.add)
 
+        def te_turn(v):
+            xt = tb_pool.tile([P, 2, P, 2], F32, name="tb")
+            for i, src in ((0, te_i), (1, te_j)):
+                words = src[:, v, :].bitcast(F32)
+                for u in (0, 1):
+                    nc.tensor.transpose(xt[:, i, :, u], words[:, u:K // 2:2], ident[:])
+            n = min(PER_TILE, N_TE_SAMPLES - PER_TILE * v)
+            for i in (0, 1):
+                nc.scalar.copy(out=te_cols[:, v % 2, 0:n, D * i:D * (i + 1), :].rearrange("p s r t -> p s (r t)").bitcast(F32),
+                               in_=xt[:, i, 0:n * D, :].rearrange("p (s r) u -> p s (r u)", s=n))
+
+        def te_turn_back(k, samples):
+            back = tb_pool.tile([P, PER_SLOT, P], BF16, name="tb")
+            v, i = divmod(samples[0], PER_TILE)
+            for s in range(PER_SLOT):
+                nc.tensor.transpose(back[:, s, :], te_cols[:, v % 2, i + s].rearrange("p r t -> p (r t)"), ident_bf[:])
+            nc.scalar.copy(out=te_rows[:, samples[0] // PER_SLOT % 4], in_=back[:])
+
+        def te_early(k, unit, samples):
+            v, i = divmod(samples[0], PER_TILE)
+            if unit == 0:
+                te_turn_back(k, samples)
+            elif i == PER_SLOT and v + 1 < N_TE_TILES:
+                te_turn(v + 1)
+
         phs = {}
 
         def te_products(k, unit, samples):
@@ -231,9 +242,7 @@ def tile_rn_pa_w4_kernel(tc, u_i, u_j, g0_b, qst_bytes, qst_scale, g1_w_words, g
             phs[(k, unit)] = ph
             for r in range(3):
                 half = 3 * unit + r
-                b = samples[half // 2]
-                nc.tensor.matmul(ph[:, 288 * r:288 * (r + 1)],
-                                 lhsT=te_rows[:, b, :].rearrange("p (m t) -> p t m", t=4)[:, 0, :],
+                nc.tensor.matmul(ph[:, 288 * r:288 * (r + 1)], lhsT=te_rows[:, samples[0] // PER_SLOT % 4, half // 2, :],
                                  rhs=sel[:, 72 * (half % 2):72 * (half % 2) + 72, :].rearrange("p n t -> p (n t)"),
                                  start=True, stop=True)
 
@@ -255,7 +264,7 @@ def tile_rn_pa_w4_kernel(tc, u_i, u_j, g0_b, qst_bytes, qst_scale, g1_w_words, g
             b = samples[0]
             n = len(samples)
             v, i = divmod(b - N_TE_SAMPLES, PER_TILE)
-            if i == 0 and v > 0:
+            if i == 0:
                 add_bias(v)
             off = b * D - ve_row0(v)
             ui_bf = xts[v][:, 0, off:off + n * D, :].rearrange("p r u -> p (r u)").bitcast(BF16)
@@ -272,21 +281,29 @@ def tile_rn_pa_w4_kernel(tc, u_i, u_j, g0_b, qst_bytes, qst_scale, g1_w_words, g
                 flat = h[:, column(k):column(k) + n, :].rearrange("p n t -> p (n t)")
                 nc.vector.tensor_scalar_max(flat, flat, 0.0)
 
+        def nothing():
+            return None
+
         items = []
         for k, (kind, samples) in enumerate(slots):
             if kind == "te":
                 for unit in (0, 1):
-                    items.append((k, lambda k=k, unit=unit, samples=samples: te_products(k, unit, samples),
+                    items.append((k, lambda k=k, unit=unit, samples=samples: te_early(k, unit, samples),
+                                  lambda k=k, unit=unit, samples=samples: te_products(k, unit, samples),
                                   lambda k=k, unit=unit: te_relu(k, unit)))
             else:
-                items.append((k, lambda samples=samples: ve_tensor(samples), lambda k=k, samples=samples: ve_sums(k, samples)))
-        state = {"tensor": 0}
+                items.append((k, nothing, lambda samples=samples: ve_tensor(samples),
+                              lambda k=k, samples=samples: ve_sums(k, samples)))
+        state = {"early": 0, "tensor": 0}
 
         def produce(n):
+            while state["early"] < min(n + 3, len(items)):
+                items[state["early"]][1]()
+                state["early"] += 1
             while state["tensor"] < min(n + 2, len(items)):
-                items[state["tensor"]][1]()
+                items[state["tensor"]][2]()
                 state["tensor"] += 1
-            items[n][2]()
+            items[n][3]()
 
         plan = quantize_plan()
 
@@ -309,15 +326,25 @@ def tile_rn_pa_w4_kernel(tc, u_i, u_j, g0_b, qst_bytes, qst_scale, g1_w_words, g
                 nc.tensor.matmul_mx(out=z[:, w:w + 256], lhsT=w_perm[:, j, :].bitcast(FP4X4), lhsT_scale=ws_perm[:, j, :],
                                     rhs=codes[:, lo:lo + 256].bitcast(FP8X4), rhs_scale=scales[:, lo:lo + 256],
                                     start=True, stop=True)
-            for s, b in enumerate(samples):
-                junk = junk_pool.tile([P, PAIRS], F32, name="junk")
-                src = z[:, s * PAIRS:(s + 1) * PAIRS]
-                if (k, j) in VEC_BANKS:
-                    nc.vector.scalar_tensor_tensor(out=junk[:], in0=src, scalar=bias[:, j, b:b + 1], in1=zeros[:],
-                                                   op0=ALU.add, op1=ALU.max, accum_out=acc[:, b, j:j + 1])
-                else:
-                    nc.scalar.activation(out=junk[:], in_=src, func=ACT.Relu, bias=bias[:, j, b:b + 1],
-                                         accum_out=acc[:, b, j:j + 1])
+            if (k, j) in VEC_BANKS:
+                deferred.append((z, j, samples))
+                if k == N_SLOTS - 1:
+                    reduce_on_vector()
+            else:
+                for s, b in enumerate(samples):
+                    junk = junk_pool.tile([P, PAIRS], F32, name="junk")
+                    nc.scalar.activation(out=junk[:], in_=z[:, s * PAIRS:(s + 1) * PAIRS], func=ACT.Relu,
+                                         bias=bias[:, j, b:b + 1], accum_out=acc[:, b, j:j + 1])
+
+        deferred = []
+
+        def reduce_on_vector():
+            for z, j, samples in deferred:
+                for s, b in enumerate(samples):
+                    junk = junk_pool.tile([P, PAIRS], F32, name="vjunk")
+                    nc.vector.scalar_tensor_tensor(out=junk[:], in0=z[:, s * PAIRS:(s + 1) * PAIRS], scalar=bias[:, j, b:b + 1],
+                                                   in1=zeros[:], op0=ALU.add, op1=ALU.max, accum_out=acc[:, b, j:j + 1])
+            deferred.clear()
 
         def question_values():
             nc.vector.tensor_tensor(out=q_val[:], in0=q_raw[:].bitcast(FP8), in1=q_scale[:], op=ALU.mult)
@@ -344,26 +371,36 @@ def tile_rn_pa_w4_kernel(tc, u_i, u_j, g0_b, qst_bytes, qst_scale, g1_w_words, g
         def finish_xg(b0, b1):
             nc.vector.tensor_copy(out=xg[:, b0:b1, :], in_=acc[:, b0:b1, :])
 
+        nc.vector.tensor_copy(out=te_cols[:, :, :, 2 * D, :].rearrange("p v s t -> p (v s) t"),
+                              in_=g0_t[:].unsqueeze(1).to_broadcast([P, 2 * PER_TILE, 4]))
+        te_turn(0)
+        nc.vector.tensor_copy(out=w_perm[:].rearrange("p j (m e) -> p j m e", e=2),
+                              in_=w_raw[:, 0].rearrange("p (m j e) -> p j m e", j=4, e=2))
         question_values()
+        items[0][1]()
+        items[1][1]()
+        items[0][2]()
+        state["early"] = 2
+        state["tensor"] = 1
         question_turn()
-        turn_rows(0)
-        add_bias(0)
+        items[1][2]()
+        state["tensor"] = 2
+        items[0][3]()
+        items[1][3]()
         question_product()
-        nc.vector.tensor_copy(out=ws_perm[:], in_=ws_raw[:, 0].rearrange("p (m j) -> p j m", j=4))
-        produce(0)
-        relu(0)
         next_piece = 0
         while last_slot(next_piece) <= 0:
             quantize(next_piece)
             next_piece += 1
-        make_sel()
+        nc.vector.tensor_copy(out=ws_perm[:], in_=ws_raw[:, 0].rearrange("p (m j) -> p j m", j=4))
+        turn_rows(0)
 
         produced = 0
-        next_item = 1
+        next_item = 2
         relued = 0
         early_te = early_ve = 0
         for k in range(N_SLOTS):
-            target = min(k + LEAD, 1 + 2 * k, N_SLOTS - 1)
+            target = min(k + LEAD, max(k + 1, 2 * k + 2 - RAMP), N_SLOTS - 1)
             before = produced
             produced = target
             end = next_item
@@ -371,12 +408,13 @@ def tile_rn_pa_w4_kernel(tc, u_i, u_j, g0_b, qst_bytes, qst_scale, g1_w_words, g
                 end += 1
             todo = range(next_item, end)
             next_item = end
-            relu_to = target - 1 if k >= LEAD and target < N_SLOTS - 1 else target
+            relu_to = target - 1 if target >= k + 3 and target < N_SLOTS - 1 else target
             for j in range(4):
                 z_and_reduce(k, j)
                 for n in todo[len(todo) * j // 4:len(todo) * (j + 1) // 4]:
                     produce(n)
                 if j == 1:
+                    reduce_on_vector()
                     while next_piece < len(plan) and last_slot(next_piece) <= relued:
                         quantize(next_piece)
                         next_piece += 1

from contextlib import ExitStack

import concourse.mybir as mybir
from concourse.masks import make_identity

F32 = mybir.dt.float32
BF16 = mybir.dt.bfloat16
I32 = mybir.dt.int32
U32 = mybir.dt.uint32
U8 = mybir.dt.uint8
FP8 = mybir.dt.float8_e4m3fn
FP8X4 = mybir.dt.float8_e4m3fn_x4
FP4X4 = mybir.dt.float4_e2m1fn_x4
ALU = mybir.AluOpType
ACT = mybir.ActivationFunctionType

P = 128
B, D, K = 128, 12, 512
PAIRS = D * D
ROWS = B * PAIRS
FLOPS = 2 * ROWS * K * K + 2 * (2 * B * K * K)

PER_SLOT = 3
SLOT = 448
BLOCK = 8 * SLOT
N_SLOTS = 43
N_TE = 17
N_TE_SAMPLES = N_TE * PER_SLOT
PER_TILE = 9
N_TILES = 9
LEAD = 4
RAMP = 0
VEC_BANKS = [(k, 3) for k in range(8, 39) if k % 3 == 1] + [(39, 1), (39, 3), (40, 1), (40, 3), (41, 1), (41, 3), (42, 1), (42, 3)]
SCALAR_UNITS = []
N_TE_TILES = 6
Z_BANKS = 3


def slot_plan():
    te = [("te", [PER_SLOT * i + s for s in range(PER_SLOT)]) for i in range(N_TE)]
    ve = []
    b = N_TE_SAMPLES
    while b < B:
        ve.append(("ve", list(range(b, min(b + PER_SLOT, B)))))
        b += PER_SLOT
    order = []
    n_te, n_ve = 0, 0
    while n_te + n_ve < N_SLOTS:
        if n_te < N_TE and n_te * len(ve) <= n_ve * N_TE + 0:
            order.append(te[n_te])
            n_te += 1
        else:
            order.append(ve[n_ve])
            n_ve += 1
    return order


def quantize_plan():
    widths = [256, 128, 64] * 4 + [512] * 3 + [256]
    widths += [512] * (4 * 7) + [512, 512, 256]
    plan, at = [], 0
    for w in widths:
        plan.append((at, w))
        at += w
    return plan


def tile_rn_pa_w4_kernel(tc, u_i, u_j, g0_b, qst_bytes, qst_scale, g1_w_words, g1_w_scales, g1_b,
                                     f1_w_words, f1_w_scales, f1_b, out):
    nc = tc.nc
    with ExitStack() as ctx:
        keep = ctx.enter_context(tc.tile_pool(name="keep", bufs=1))
        junk_pool = ctx.enter_context(tc.tile_pool(name="junk_pool", bufs=6))
        z_pool = ctx.enter_context(tc.psum_pool(name="z_pool", bufs=Z_BANKS))
        tb_pool = ctx.enter_context(tc.psum_pool(name="tb_pool", bufs=1))
        ph_pool = ctx.enter_context(tc.psum_pool(name="ph_pool", bufs=2))
        xt_pool = ctx.enter_context(tc.psum_pool(name="xt_pool", bufs=2))
        ctx.enter_context(tc.manual_schedule())

        ui_rows = u_i.rearrange("b d k -> (b d) k")
        uj_rows = u_j.rearrange("b d k -> (b d) k")

        te_i = keep.tile([P, N_TE_TILES, K], BF16, align_bytes=64)
        te_j = keep.tile([P, N_TE_TILES, K], BF16, align_bytes=64)
        te_cols = keep.tile([P, 2, PER_TILE, 32, 4], BF16, align_bytes=64)
        te_rows = keep.tile([P, 4, PER_SLOT, P], BF16, align_bytes=64)
        ve_i = keep.tile([P, N_TILES, K], BF16, align_bytes=64)
        ve_j = keep.tile([P, N_TILES, K], BF16, align_bytes=64)
        g0_t = keep.tile([P, 4], BF16, align_bytes=64)
        g1_t = keep.tile([P, 4], BF16, align_bytes=64)
        q_raw = keep.tile([P, K], U8, align_bytes=64)
        q_scale = keep.tile([P, K], F32, align_bytes=64)
        w_raw = keep.tile([P, 2, 1024], U8, align_bytes=64)
        ws_raw = keep.tile([P, 2, K], U8, align_bytes=64)
        w_perm = keep.tile([P, 4, 256], U8, align_bytes=64)
        ws_perm = keep.tile([P, 4, P], U8, align_bytes=64)
        f1_words = keep.tile([P, 1024], U8, align_bytes=64)
        f1_scales = keep.tile([P, K], U8, align_bytes=64)
        f1_bias = keep.tile([P, K], BF16, align_bytes=64)
        ident = keep.tile([P, P], F32, align_bytes=64)
        ident_bf = keep.tile([P, P], BF16, align_bytes=64)
        sel = keep.tile([P, PAIRS, 4], BF16, align_bytes=64)
        zeros = keep.tile([P, PAIRS], F32, align_bytes=64)
        h = keep.tile([P, 2 * BLOCK, 4], BF16, align_bytes=64)
        codes = keep.tile([P, 2 * BLOCK], U32, align_bytes=64)
        scales = keep.tile([P, 2 * BLOCK], U8, align_bytes=64)
        ujg = keep.tile([P, 2, PER_TILE * D, 4], F32, align_bytes=64)
        bias = keep.tile([P, 4, B], F32, align_bytes=64)
        acc = keep.tile([P, B, 4], F32, align_bytes=64)
        xg = keep.tile([P, B, 4], BF16, align_bytes=64)
        xg_codes = keep.tile([P, B], U32, align_bytes=64)
        xg_scales = keep.tile([P, B], U8, align_bytes=64)
        result = keep.tile([P, K], F32, align_bytes=64)
        q_val = keep.tile([P, K], BF16, align_bytes=64)
        q_prod = keep.tile([P, K], F32, align_bytes=64)
        q_int = keep.tile([P, K], BF16, align_bytes=64)
        q_codes = keep.tile([P, B], U32, align_bytes=64)
        q_scales = keep.tile([P, B], U8, align_bytes=64)
        warm = keep.tile([P, 1], F32)

        nc.vector.memset(ws_raw[:].rearrange("p g n -> p (g n)").bitcast(I32), 0)
        make_identity(nc, ident[:])
        nc.gpsimd.memset(f1_scales[:].bitcast(I32), 0)

        def load_te(v, queue):
            r0 = PER_TILE * D * v
            queue.dma_start(out=te_i[:, v, :], in_=ui_rows[r0:r0 + P, :])
            queue.dma_start(out=te_j[:, v, :], in_=uj_rows[r0:r0 + P, :])

        def ve_row0(v):
            return min((N_TE_SAMPLES + PER_TILE * v) * D, B * D - P)

        def load_ve(v, queue):
            r0 = ve_row0(v)
            queue.dma_start(out=ve_j[:, v, :], in_=uj_rows[r0:r0 + P, :])
            queue.dma_start(out=ve_i[:, v, :], in_=ui_rows[r0:r0 + P, :])

        load_te(0, nc.scalar)
        nc.sync.dma_start(out=g0_t[:], in_=g0_b.rearrange("(p t) -> p t", t=4))
        nc.sync.dma_start(out=w_raw[:].bitcast(I32), in_=g1_w_words.rearrange("g p n -> p g n").bitcast(I32))
        nc.sync.dma_start(out=q_raw[:], in_=qst_bytes)
        nc.sync.dma_start(out=q_scale[:], in_=qst_scale.rearrange("o k -> (o k)").partition_broadcast(P))
        for q in range(4):
            nc.sync.dma_start(out=ws_raw[32 * q:32 * q + 4, :, :].bitcast(I32),
                              in_=g1_w_scales[:, 4 * q:4 * q + 4, :].rearrange("g r n -> r g n").bitcast(I32))
        nc.scalar.activation(out=warm[:], in_=ident[:, 0:1], func=ACT.Relu)
        load_ve(0, nc.sync)
        nc.sync.dma_start(out=g1_t[:], in_=g1_b.rearrange("(p t) -> p t", t=4))
        load_ve(1, nc.sync)
        load_te(1, nc.sync)
        load_ve(2, nc.sync)
        load_te(2, nc.sync)
        load_ve(3, nc.sync)
        load_te(3, nc.sync)
        load_ve(4, nc.sync)
        load_te(4, nc.sync)
        load_ve(5, nc.sync)
        load_te(5, nc.sync)
        for v in range(6, N_TILES):
            load_ve(v, nc.sync)
        for q in range(4):
            nc.sync.dma_start(out=f1_scales[32 * q:32 * q + 4, :].bitcast(I32),
                              in_=f1_w_scales[0, 4 * q:4 * q + 4, :].bitcast(I32))
        nc.sync.dma_start(out=f1_words[:].bitcast(I32), in_=f1_w_words[0].bitcast(I32))
        nc.sync.dma_start(out=f1_bias[:], in_=f1_b.partition_broadcast(P))

        nc.vector.memset(h[:].rearrange("p (s n) t -> p s (n t)", n=SLOT)[:, :, PER_SLOT * PAIRS * 4:], 0.0)

        nc.vector.tensor_copy(out=ident_bf[:], in_=ident[:])
        by_t = ident_bf[:].rearrange("p (r t) -> p r t", t=4)
        nc.vector.memset(te_cols[:, :, :, 2 * D + 1:, :].rearrange("p v s r t -> p (v s) (r t)"), 0.0)
        nc.vector.tensor_tensor(out=sel[:].rearrange("p (a c) t -> p a c t", a=D),
                                in0=by_t[:, 0:D, :].unsqueeze(1).to_broadcast([P, D, D, 4]),
                                in1=by_t[:, D:2 * D, :].unsqueeze(2).to_broadcast([P, D, D, 4]), op=ALU.add)
        nc.vector.memset(zeros[:], 0.0)
        nc.vector.tensor_tensor(out=sel[:], in0=sel[:], in1=by_t[:, 2 * D, :].unsqueeze(1).to_broadcast([P, PAIRS, 4]),
                                op=ALU.add)

        slots = slot_plan()
        assert len(slots) == N_SLOTS

        def column(k):
            return (k // 8) % 2 * BLOCK + k % 8 * SLOT

        slot_of = {}
        for k, (kind, samples) in enumerate(slots):
            for s, b in enumerate(samples):
                slot_of[b] = column(k) + s * PAIRS

        xts = {}

        def tile_samples(v):
            b0 = N_TE_SAMPLES + PER_TILE * v
            return list(range(b0, min(b0 + PER_TILE, B)))

        def turn_rows(v):
            xt = xt_pool.tile([P, 2, P, 2], F32, name="xt")
            xts[v] = xt
            for i, src in ((1, ve_j), (0, ve_i)):
                words = src[:, v, :].bitcast(F32)
                for u in (0, 1):
                    nc.tensor.transpose(xt[:, i, :, u], words[:, u:K // 2:2], ident[:])

        def add_bias(v):
            samples = tile_samples(v)
            off = samples[0] * D - ve_row0(v)
            n = len(samples) * D
            nc.vector.tensor_tensor(
                out=ujg[:, v % 2, 0:n, :],
                in0=xts[v][:, 1, off:off + n, :].rearrange("p r u -> p (r u)").bitcast(BF16).rearrange("p (r t) -> p r t", t=4),
                in1=g0_t[:].unsqueeze(1).to_broadcast([P, n, 4]), op=ALU.add)

        def te_turn(v):
            xt = tb_pool.tile([P, 2, P, 2], F32, name="tb")
            for i, src in ((0, te_i), (1, te_j)):
                words = src[:, v, :].bitcast(F32)
                for u in (0, 1):
                    nc.tensor.transpose(xt[:, i, :, u], words[:, u:K // 2:2], ident[:])
            n = min(PER_TILE, N_TE_SAMPLES - PER_TILE * v)
            for i in (0, 1):
                nc.scalar.copy(out=te_cols[:, v % 2, 0:n, D * i:D * (i + 1), :].rearrange("p s r t -> p s (r t)").bitcast(F32),
                               in_=xt[:, i, 0:n * D, :].rearrange("p (s r) u -> p s (r u)", s=n))

        def te_turn_back(k, samples):
            back = tb_pool.tile([P, PER_SLOT, P], BF16, name="tb")
            v, i = divmod(samples[0], PER_TILE)
            for s in range(PER_SLOT):
                nc.tensor.transpose(back[:, s, :], te_cols[:, v % 2, i + s].rearrange("p r t -> p (r t)"), ident_bf[:])
            nc.scalar.copy(out=te_rows[:, samples[0] // PER_SLOT % 4], in_=back[:])

        def te_early(k, unit, samples):
            v, i = divmod(samples[0], PER_TILE)
            if unit == 0:
                te_turn_back(k, samples)
            elif i == PER_SLOT and v + 1 < N_TE_TILES:
                te_turn(v + 1)

        phs = {}

        def te_products(k, unit, samples):
            ph = ph_pool.tile([P, 1024], BF16, name="ph")
            phs[(k, unit)] = ph
            for r in range(3):
                half = 3 * unit + r
                nc.tensor.matmul(ph[:, 288 * r:288 * (r + 1)], lhsT=te_rows[:, samples[0] // PER_SLOT % 4, half // 2, :],
                                 rhs=sel[:, 72 * (half % 2):72 * (half % 2) + 72, :].rearrange("p n t -> p (n t)"),
                                 start=True, stop=True)

        def te_relu(k, unit):
            ph = phs.pop((k, unit))
            lo = column(k) + 216 * unit
            dst = h[:, lo:lo + 216, :].rearrange("p n t -> p (n t)")
            if (k, unit) in SCALAR_UNITS:
                nc.scalar.activation(out=dst, in_=ph[:, 0:864], func=ACT.Relu)
            else:
                nc.vector.tensor_scalar_max(dst, ph[:, 0:864], 0.0)

        def ve_tensor(samples):
            v, i = divmod(samples[0] - N_TE_SAMPLES, PER_TILE)
            if i == 2 * PER_SLOT and v + 1 < N_TILES:
                turn_rows(v + 1)

        def ve_sums(k, samples):
            b = samples[0]
            n = len(samples)
            v, i = divmod(b - N_TE_SAMPLES, PER_TILE)
            if i == 0:
                add_bias(v)
            off = b * D - ve_row0(v)
            ui_bf = xts[v][:, 0, off:off + n * D, :].rearrange("p r u -> p (r u)").bitcast(BF16)
            nc.vector.tensor_tensor(
                out=h[:, column(k):column(k) + n * PAIRS, :].rearrange("p (s a c) t -> p s a c t", s=n, a=D),
                in0=ui_bf.rearrange("p (s c t) -> p s c t", c=D, t=4).unsqueeze(2).to_broadcast([P, n, D, D, 4]),
                in1=ujg[:, v % 2, i * D:(i + n) * D, :].rearrange("p (s a) t -> p s a t", a=D).unsqueeze(3).to_broadcast(
                    [P, n, D, D, 4]),
                op=ALU.add)

        def relu(k):
            if slots[k][0] == "ve":
                n = len(slots[k][1]) * PAIRS
                flat = h[:, column(k):column(k) + n, :].rearrange("p n t -> p (n t)")
                nc.vector.tensor_scalar_max(flat, flat, 0.0)

        def nothing():
            return None

        items = []
        for k, (kind, samples) in enumerate(slots):
            if kind == "te":
                for unit in (0, 1):
                    items.append((k, lambda k=k, unit=unit, samples=samples: te_early(k, unit, samples),
                                  lambda k=k, unit=unit, samples=samples: te_products(k, unit, samples),
                                  lambda k=k, unit=unit: te_relu(k, unit)))
            else:
                items.append((k, nothing, lambda samples=samples: ve_tensor(samples),
                              lambda k=k, samples=samples: ve_sums(k, samples)))
        state = {"early": 0, "tensor": 0}

        def produce(n):
            while state["early"] < min(n + 3, len(items)):
                items[state["early"]][1]()
                state["early"] += 1
            while state["tensor"] < min(n + 2, len(items)):
                items[state["tensor"]][2]()
                state["tensor"] += 1
            items[n][3]()

        plan = quantize_plan()

        def quantize(piece):
            at, width = plan[piece]
            lo = at // BLOCK % 2 * BLOCK + at % BLOCK
            nc.vector.quantize_mx(out=codes[:, lo:lo + width].bitcast(FP8X4), scales=scales[:, lo:lo + width],
                                  in_=h[:, lo:lo + width, :].rearrange("p n t -> p (n t)"))

        def last_slot(piece):
            at, width = plan[piece]
            return min((at + width - 1) // SLOT, N_SLOTS - 1)

        def z_and_reduce(k, j):
            samples = slots[k][1]
            z = z_pool.tile([P, 512], F32, name="z")
            second = 192 if len(samples) == PER_SLOT else 64
            for w in (0, second):
                lo = column(k) + w
                nc.tensor.matmul_mx(out=z[:, w:w + 256], lhsT=w_perm[:, j, :].bitcast(FP4X4), lhsT_scale=ws_perm[:, j, :],
                                    rhs=codes[:, lo:lo + 256].bitcast(FP8X4), rhs_scale=scales[:, lo:lo + 256],
                                    start=True, stop=True)
            if (k, j) in VEC_BANKS:
                deferred.append((z, j, samples))
                if k == N_SLOTS - 1:
                    reduce_on_vector()
            else:
                for s, b in enumerate(samples):
                    junk = junk_pool.tile([P, PAIRS], F32, name="junk")
                    nc.scalar.activation(out=junk[:], in_=z[:, s * PAIRS:(s + 1) * PAIRS], func=ACT.Relu,
                                         bias=bias[:, j, b:b + 1], accum_out=acc[:, b, j:j + 1])

        deferred = []

        def reduce_on_vector():
            for z, j, samples in deferred:
                for s, b in enumerate(samples):
                    junk = junk_pool.tile([P, PAIRS], F32, name="vjunk")
                    nc.vector.scalar_tensor_tensor(out=junk[:], in0=z[:, s * PAIRS:(s + 1) * PAIRS], scalar=bias[:, j, b:b + 1],
                                                   in1=zeros[:], op0=ALU.add, op1=ALU.max, accum_out=acc[:, b, j:j + 1])
            deferred.clear()

        def question_values():
            nc.vector.tensor_tensor(out=q_val[:], in0=q_raw[:].bitcast(FP8), in1=q_scale[:], op=ALU.mult)

        def question_turn():
            xq = xt_pool.tile([P, 2, P, 2], F32, name="xt")
            words = q_val[:].bitcast(F32)
            for u in (0, 1):
                nc.tensor.transpose(xq[:, 0, :, u], words[:, u:K // 2:2], ident[:])
            nc.scalar.copy(out=q_int[:].bitcast(F32), in_=xq[:, 0].rearrange("p r u -> p (r u)"))

        def question_product():
            nc.vector.quantize_mx(out=q_codes[:].bitcast(FP8X4), scales=q_scales[:], in_=q_int[:])
            zq = z_pool.tile([P, 512], F32, name="z")
            nc.tensor.matmul_mx(out=zq[:], lhsT=q_codes[:].bitcast(FP8X4), lhsT_scale=q_scales[:],
                                rhs=w_raw[:, 1, :].bitcast(FP4X4), rhs_scale=ws_raw[:, 1, :], start=True, stop=True)
            nc.scalar.copy(out=q_prod[:], in_=zq[:])
            zqt = z_pool.tile([P, 512], F32, name="z")
            for j in range(4):
                nc.tensor.transpose(zqt[:, j * P:(j + 1) * P], q_prod[:].rearrange("p (m j) -> p j m", j=4)[:, j, :], ident[:])
            for j in range(4):
                nc.scalar.activation(out=bias[:, j, :], in_=zqt[:, j * P:(j + 1) * P], func=ACT.Identity, bias=g1_t[:, j:j + 1])

        def finish_xg(b0, b1):
            nc.vector.tensor_copy(out=xg[:, b0:b1, :], in_=acc[:, b0:b1, :])

        nc.vector.tensor_copy(out=te_cols[:, :, :, 2 * D, :].rearrange("p v s t -> p (v s) t"),
                              in_=g0_t[:].unsqueeze(1).to_broadcast([P, 2 * PER_TILE, 4]))
        te_turn(0)
        nc.vector.tensor_copy(out=w_perm[:].rearrange("p j (m e) -> p j m e", e=2),
                              in_=w_raw[:, 0].rearrange("p (m j e) -> p j m e", j=4, e=2))
        question_values()
        items[0][1]()
        items[1][1]()
        items[0][2]()
        state["early"] = 2
        state["tensor"] = 1
        question_turn()
        items[1][2]()
        state["tensor"] = 2
        items[0][3]()
        items[1][3]()
        question_product()
        next_piece = 0
        while last_slot(next_piece) <= 0:
            quantize(next_piece)
            next_piece += 1
        nc.vector.tensor_copy(out=ws_perm[:], in_=ws_raw[:, 0].rearrange("p (m j) -> p j m", j=4))
        turn_rows(0)

        produced = 0
        next_item = 2
        relued = 0
        early_te = early_ve = 0
        for k in range(N_SLOTS):
            target = min(k + LEAD, max(k + 1, 2 * k + 2 - RAMP), N_SLOTS - 1)
            before = produced
            produced = target
            end = next_item
            while end < len(items) and items[end][0] <= produced:
                end += 1
            todo = range(next_item, end)
            next_item = end
            relu_to = target - 1 if target >= k + 3 and target < N_SLOTS - 1 else target
            for j in range(4):
                z_and_reduce(k, j)
                for n in todo[len(todo) * j // 4:len(todo) * (j + 1) // 4]:
                    produce(n)
                if j == 1:
                    reduce_on_vector()
                    while next_piece < len(plan) and last_slot(next_piece) <= relued:
                        quantize(next_piece)
                        next_piece += 1
                    while relued < before:
                        relued += 1
                        relu(relued)
            while relued < relu_to:
                relued += 1
                relu(relued)
            while (next_piece < len(plan) and last_slot(next_piece) <= relued
                   and plan[next_piece][0] < (k + 2) * SLOT):
                quantize(next_piece)
                next_piece += 1
            assert k + 1 >= N_SLOTS or next_piece == len(plan) or plan[next_piece][0] >= (k + 2) * SLOT
            if k == N_SLOTS - 4:
                early_te = sum(len(s) for kind, s in slots[0:k] if kind == "te")
                early_ve = N_TE_SAMPLES + sum(len(s) for kind, s in slots[0:k] if kind == "ve")
                finish_xg(0, early_te)
                finish_xg(N_TE_SAMPLES, early_ve)

        if early_te < N_TE_SAMPLES:
            finish_xg(early_te, N_TE_SAMPLES)
        finish_xg(early_ve, B)
        nc.vector.quantize_mx(out=xg_codes[:].bitcast(FP8X4), scales=xg_scales[:], in_=xg[:].rearrange("p b t -> p (b t)"))
        y = z_pool.tile([P, 512], F32, name="z")
        nc.tensor.matmul_mx(out=y[:], lhsT=xg_codes[:].bitcast(FP8X4), lhsT_scale=xg_scales[:],
                            rhs=f1_words[:].bitcast(FP4X4), rhs_scale=f1_scales[:], start=True, stop=True)
        for c in (0, 1):
            cols = slice(c * 256, (c + 1) * 256)
            nc.vector.tensor_tensor(out=result[:, cols], in0=y[:, cols], in1=f1_bias[:, cols], op=ALU.add)
            nc.scalar.activation(out=result[:, cols], in_=result[:, cols], func=ACT.Relu)
            nc.sync.dma_start(out=out[:, cols], in_=result[:, cols])
